import numpy as np
import ml_dtypes


def mxq(x, axis, fmt="e4m3"):
    dtype, down = {"e4m3": (ml_dtypes.float8_e4m3fn, 7), "e5m2": (ml_dtypes.float8_e5m2, 14)}[fmt]
    v = np.moveaxis(np.asarray(x, np.float32).astype(ml_dtypes.bfloat16).astype(np.float64), axis, -1)
    blocks = v.reshape(v.shape[:-1] + (-1, 32))
    amax = np.abs(blocks).max(-1, keepdims=True)
    byte = np.maximum(np.where(amax > 0, np.frexp(amax)[1] - 1 + 127, 0) - down, 1)
    scale = np.exp2(byte - 127.0)
    codes = (blocks / scale).astype(np.float32).astype(dtype).astype(np.float64)
    return np.moveaxis((codes * scale).reshape(v.shape), -1, axis)


WIDE = False


def mx_kscale(k):
    if not WIDE:
        return np.ones(k)
    levels = np.array([10, -10, 5, -5, 0])
    a = np.random.permutation(np.resize(levels, k // 512 * 4)).reshape(k // 512, 4)
    idx = np.arange(k)
    return np.exp2(a[idx // 512, idx % 128 // 32])


BF16 = ml_dtypes.bfloat16


def bf(x):
    return np.asarray(x, np.float32).astype(BF16)


def f64(x):
    return np.asarray(x).astype(np.float64)


B, H, HKV, S, D = 8, 4, 2, 512, 256
G = H // HKV
NEG = -1e9


def setup_inputs():
    s = mx_kscale(S)
    keep = np.random.random((B, 1, S, S)) < 0.75
    return {"query": bf(np.random.standard_normal((B, H, S, D))),
            "key": bf(np.random.standard_normal((B, HKV, S, D))),
            "value": bf(np.random.standard_normal((B, HKV, S, D)) * 0.25 * np.sqrt(S) * s.max() / s[:, None]),
            "attention_mask": bf(np.where(keep, 0.5 * np.random.standard_normal((B, 1, S, S)) + np.log(s), NEG)),
            "sinks": bf(np.log(S * s.max()) - 3.5 + np.random.standard_normal(H))}


def reference(query, key, value, attention_mask, sinks):
    scaling = 1.0 / np.sqrt(D)
    k = np.repeat(f64(key), G, axis=1)
    attn = (f64(query) @ k.transpose(0, 1, 3, 2)) * scaling
    attn = attn + f64(attention_mask)[:, :, :, :attn.shape[-1]]
    sink_col = np.broadcast_to(f64(sinks).reshape(1, H, 1, 1), (B, H, S, 1))
    combined = np.concatenate([attn, sink_col], axis=-1)
    combined = combined - combined.max(-1, keepdims=True)
    e = np.exp(combined[..., :-1])
    den = e.sum(-1, keepdims=True) + np.exp(combined[..., -1:])
    eg = e.reshape(B, HKV, G * S, S)
    pv = mxq(eg, 3, "e4m3") @ mxq(f64(value), 2, "e4m3")
    out = pv.reshape(B, H, S, D) / den
    return out.transpose(0, 2, 1, 3)

@@ -1,0 +1,248 @@
+from contextlib import ExitStack
+
+import concourse.bass as bass
+import concourse.mybir as mybir
+import concourse.tile as tile
+from concourse.masks import make_identity
+
+F32 = mybir.dt.float32
+BF16 = mybir.dt.bfloat16
+U32 = mybir.dt.uint32
+U8 = mybir.dt.uint8
+FP8X4 = mybir.dt.float8_e4m3fn_x4
+ALU = mybir.AluOpType
+ACT = mybir.ActivationFunctionType
+AX = mybir.AxisListType
+
+B, H, HKV, S, D = 8, 4, 2, 512, 256
+G = H // HKV
+P = 128
+NT = S // P
+W = D // 2
+FLOPS = 2 * 2 * B * H * S * S * D
+DUOS_PER_BATCH = H * NT // 2
+N_DUOS = B * DUOS_PER_BATCH
+
+
+def tile_deepseekv4attention_t_kernel(tc, query, key, value, attention_mask, sinks, out):
+    nc = tc.nc
+    with ExitStack() as ctx:
+        const = ctx.enter_context(tc.tile_pool(name="const", bufs=1))
+        ld = ctx.enter_context(tc.tile_pool(name="ld", bufs=3))
+        prep = ctx.enter_context(tc.tile_pool(name="prep", bufs=2))
+        prep3 = ctx.enter_context(tc.tile_pool(name="prep3", bufs=3))
+        work = ctx.enter_context(tc.tile_pool(name="work", bufs=3))
+        stat = ctx.enter_context(tc.tile_pool(name="stat", bufs=6))
+        outp = ctx.enter_context(tc.tile_pool(name="outp", bufs=3))
+        ps_sc = ctx.enter_context(tc.psum_pool(name="ps_sc", bufs=3))
+        ps_et = ctx.enter_context(tc.psum_pool(name="ps_et", bufs=2))
+        ps_o = ctx.enter_context(tc.psum_pool(name="ps_o", bufs=2))
+        ps_tq = ctx.enter_context(tc.psum_pool(name="ps_tq", bufs=1))
+
+        ident_f = const.tile([P, P], F32)
+        make_identity(nc, ident_f[:])
+        ident_b = const.tile([P, P], BF16)
+        make_identity(nc, ident_b[:])
+        sink_raw = const.tile([P, H], BF16)
+        nc.sync.dma_start(out=sink_raw[:], in_=sinks.partition_broadcast(P))
+        sink_f = const.tile([P, H], F32)
+        nc.vector.tensor_copy(out=sink_f[:], in_=sink_raw[:])
+        sink16 = const.tile([P, H], F32)
+        nc.vector.tensor_scalar(out=sink16[:], in0=sink_raw[:], scalar1=16.0, scalar2=None, op0=ALU.mult)
+
+        loaded = {}
+        ready = {}
+
+        def load(b):
+            k_sb = ld.tile([P, HKV * NT * D], BF16, tag="k_sb")
+            nc.sync.dma_start(
+                out=k_sb[:].rearrange("p (x d) -> p x d", d=D),
+                in_=key[b].rearrange("g (t p) d -> p (g t) d", p=P),
+            )
+            q_sb = ld.tile([P, H * NT * D], BF16, tag="q_sb")
+            nc.sync.dma_start(
+                out=q_sb[:].rearrange("p (h x) -> p h x", h=H),
+                in_=query[b].rearrange("h (p t) d -> p h (t d)", t=NT),
+            )
+            m_sb = ld.tile([P, NT * S], BF16, tag="m_sb")
+            nc.sync.dma_start(out=m_sb[:], in_=attention_mask[b, 0].rearrange("(p t) k -> p (t k)", t=NT))
+            v_sb = ld.tile([P, HKV * NT * D], BF16, tag="v_sb")
+            nc.sync.dma_start(
+                out=v_sb[:].rearrange("p (x d) -> p x d", d=D),
+                in_=value[b].rearrange("g (t p) d -> p (g t) d", p=P),
+            )
+            loaded[b] = (q_sb, k_sb, v_sb, m_sb)
+
+        def prep_alloc(b):
+            qT = prep.tile([P, H * NT * P], F32, tag="qT")
+            kT = prep.tile([P, HKV * NT * P], F32, tag="kT")
+            m16 = prep.tile([P, NT * S], BF16, tag="m16")
+            vc = prep3.tile([P, HKV * D], U32, tag="vc", align_bytes=64)
+            vs = prep3.tile([P, HKV * D], U8, tag="vs", align_bytes=64)
+            ready[b] = (qT, kT, m16, vc, vs)
+
+        def prep_words(src, dst, blk):
+            tq = ps_tq.tile([P, NT, P], F32, tag="tq")
+            for t in range(NT):
+                c0 = (blk * NT + t) * W
+                nc.tensor.transpose(tq[:, t, :], src[:].bitcast(F32)[:, c0 : c0 + W], ident_f[:])
+            nc.scalar.copy(out=dst[:, blk * NT * P : (blk + 1) * NT * P], in_=tq[:].rearrange("p t q -> p (t q)"))
+
+        def prep_mask_value(b):
+            q_sb, k_sb, v_sb, m_sb = loaded[b]
+            qT, kT, m16, vc, vs = ready[b]
+            nc.gpsimd.tensor_scalar(out=m16[:], in0=m_sb[:], scalar1=16.0, scalar2=0.0, op0=ALU.mult, op1=ALU.add)
+            vg = prep.tile([P, HKV * D * NT], BF16, tag="vg", align_bytes=64)
+            nc.vector.tensor_copy(
+                out=vg[:].rearrange("p (g d t) -> p g d t", g=HKV, t=NT),
+                in_=v_sb[:].rearrange("p (g t d) -> p g d t", g=HKV, t=NT),
+            )
+            nc.vector.quantize_mx(out=vc[:].bitcast(FP8X4), scales=vs[:], in_=vg[:])
+
+        def prep_chunk(b, j):
+            if b >= B:
+                return
+            if j == 0:
+                prep_alloc(b)
+            q_sb, k_sb, v_sb, m_sb = loaded[b]
+            qT, kT, m16, vc, vs = ready[b]
+            if j == 0:
+                prep_words(k_sb, kT, 0)
+            elif j == 1:
+                prep_words(q_sb, qT, 0)
+            elif j == 2:
+                prep_words(q_sb, qT, 1)
+            elif j == 3:
+                prep_words(k_sb, kT, 1)
+            elif j == 4:
+                prep_mask_value(b)
+            elif j == 5:
+                prep_words(q_sb, qT, 2)
+            elif j == 6:
+                prep_words(q_sb, qT, 3)
+
+        st = {}
+
+        def where(n):
+            b, j = divmod(n, DUOS_PER_BATCH)
+            tp, h = divmod(j, H)
+            return b, tp, h
+
+        def stage_a(n):
+            b, tp, h = where(n)
+            g = h // G
+            qT, kT, m16, vc, vs = ready[b]
+            qTb = qT[:].bitcast(BF16).rearrange("p (c e) -> p c e", e=2)
+            kTb = kT[:].bitcast(BF16).rearrange("p (c e) -> p c e", e=2)
+            s16 = work.tile([P, 2, S], F32, tag="s16")
+            for i in range(2):
+                t = 2 * tp + i
+                sc = ps_sc.tile([P, S], F32, tag="sc")
+                c0 = (h * NT + t) * P
+                for e in range(2):
+                    nc.tensor.matmul(
+                        sc[:],
+                        lhsT=qTb[:, c0 : c0 + P, e],
+                        rhs=kTb[:, g * S : (g + 1) * S, e],
+                        start=(e == 0),
+                        stop=(e == 1),
+                    )
+                nc.vector.tensor_tensor(out=s16[:, i, :], in0=sc[:], in1=m16[:, t * S : (t + 1) * S], op=ALU.add)
+            mx = stat.tile([P, 2], F32, tag="mx")
+            nc.vector.tensor_reduce(out=mx[:], in_=s16[:], axis=AX.X, op=ALU.max)
+            negm = stat.tile([P, 2], F32, tag="negm")
+            nc.vector.tensor_scalar(
+                out=negm[:], in0=mx[:], scalar1=sink16[:, h : h + 1], scalar2=-1.0 / 16.0, op0=ALU.max, op1=ALU.mult
+            )
+            st[n] = {"s16": s16, "negm": negm}
+
+        def stage_b(n):
+            b, tp, h = where(n)
+            s16 = st[n]["s16"]
+            negm = st[n]["negm"]
+            e_sb = work.tile([P, 2, S], BF16, tag="e_sb")
+            rsum = stat.tile([P, 2], F32, tag="rsum")
+            for i in range(2):
+                nc.scalar.activation(
+                    out=e_sb[:, i, :],
+                    in_=s16[:, i, :],
+                    func=ACT.Exp,
+                    bias=negm[:, i : i + 1],
+                    scale=1.0 / 16.0,
+                    accum_out=rsum[:, i : i + 1],
+                )
+            sterm = stat.tile([P, 2], F32, tag="sterm")
+            nc.scalar.activation(out=sterm[:], in_=negm[:], func=ACT.Exp, bias=sink_f[:, h : h + 1], scale=1.0)
+            den = stat.tile([P, 2], F32, tag="den")
+            nc.vector.tensor_tensor(out=den[:], in0=rsum[:], in1=sterm[:], op=ALU.add)
+            rden = stat.tile([P, 2], F32, tag="rden")
+            nc.vector.reciprocal(out=rden[:], in_=den[:])
+            et = ps_et.tile([P, 2, NT, P], BF16, tag="et")
+            for i in range(2):
+                for k in range(NT):
+                    nc.tensor.transpose(et[:, i, k, :], e_sb[:, i, k * P : (k + 1) * P], ident_b[:])
+            st[n]["et"] = et
+            st[n]["rden"] = rden
+
+        def stage_c(n):
+            et = st[n]["et"]
+            gr = work.tile([P, 2 * P * NT], BF16, tag="gr", align_bytes=64)
+            nc.scalar.copy(
+                out=gr[:].rearrange("p (i q k) -> p i q k", i=2, k=NT),
+                in_=et[:].rearrange("p i k q -> p i q k"),
+            )
+            ec = work.tile([P, 2 * P], U32, tag="ec", align_bytes=64)
+            es = work.tile([P, 2 * P], U8, tag="es", align_bytes=64)
+            nc.vector.quantize_mx(out=ec[:].bitcast(FP8X4), scales=es[:], in_=gr[:])
+            st[n]["ec"] = ec
+            st[n]["es"] = es
+
+        osb = {}
+
+        def stage_d(n):
+            b, tp, h = where(n)
+            g = h // G
+            qT, kT, m16, vc, vs = ready[b]
+            ec = st[n]["ec"]
+            es = st[n]["es"]
+            rden = st[n]["rden"]
+            o_ps = ps_o.tile([P, 2, D], F32, tag="o_ps")
+            for i in range(2):
+                nc.tensor.matmul_mx(
+                    out=o_ps[:, i, :],
+                    lhsT=ec[:, i * P : (i + 1) * P].bitcast(FP8X4),
+                    lhsT_scale=es[:, i * P : (i + 1) * P],
+                    rhs=vc[:, g * D : (g + 1) * D].bitcast(FP8X4),
+                    rhs_scale=vs[:, g * D : (g + 1) * D],
+                    start=True,
+                    stop=True,
+                )
+            if h == 0:
+                o_sb = outp.tile([P, 2, H, D], F32, tag="o_sb")
+                osb[(b, tp)] = o_sb
+            o_sb = osb[(b, tp)]
+            for i in range(2):
+                nc.scalar.activation(out=o_sb[:, i, h, :], in_=o_ps[:, i, :], func=ACT.Copy, scale=rden[:, i : i + 1])
+            if h == H - 1:
+                nc.sync.dma_start(
+                    out=out[b].rearrange("(p t) h d -> p t (h d)", t=NT)[:, 2 * tp : 2 * tp + 2, :],
+                    in_=o_sb[:].rearrange("p i h d -> p i (h d)"),
+                )
+
+        load(0)
+        load(1)
+        for j in range(DUOS_PER_BATCH):
+            prep_chunk(0, j)
+        for n in range(N_DUOS + 3):
+            b, j = divmod(n, DUOS_PER_BATCH)
+            if n < N_DUOS:
+                if j == 0 and b + 2 < B:
+                    load(b + 2)
+                stage_a(n)
+                prep_chunk(b + 1, j)
+            if 0 <= n - 1 < N_DUOS:
+                stage_b(n - 1)
+            if 0 <= n - 2 < N_DUOS:
+                stage_c(n - 2)
+            if 0 <= n - 3 < N_DUOS:
+                stage_d(n - 3)

@@ -19,6 +19,7 @@ G = H // HKV
 P = 128
 NT = S // P
 W = D // 2
+SW = 520
 FLOPS = 2 * 2 * B * H * S * S * D
 DUOS_PER_BATCH = H * NT // 2
 N_DUOS = B * DUOS_PER_BATCH
@@ -45,10 +46,12 @@ def tile_deepseekv4attention_t_kernel(tc, query, key, value, attention_mask, sin
         make_identity(nc, ident_b[:])
         sink_raw = const.tile([P, H], BF16)
         nc.sync.dma_start(out=sink_raw[:], in_=sinks.partition_broadcast(P))
-        sink_f = const.tile([P, H], F32)
-        nc.vector.tensor_copy(out=sink_f[:], in_=sink_raw[:])
-        sink16 = const.tile([P, H], F32)
-        nc.vector.tensor_scalar(out=sink16[:], in0=sink_raw[:], scalar1=16.0, scalar2=None, op0=ALU.mult)
+        s_bufs = []
+        for h in range(H):
+            s_h = const.tile([P, 2, SW], F32, name="s_h%d" % h)
+            for i in range(2):
+                nc.vector.tensor_copy(out=s_h[:, i, S : S + 1], in_=sink_raw[:, h : h + 1])
+            s_bufs.append(s_h)
 
         loaded = {}
         ready = {}
@@ -76,27 +79,31 @@ def tile_deepseekv4attention_t_kernel(tc, query, key, value, attention_mask, sin
         def prep_alloc(b):
             qT = prep.tile([P, H * NT * P], F32, tag="qT")
             kT = prep.tile([P, HKV * NT * P], F32, tag="kT")
-            m16 = prep.tile([P, NT * S], BF16, tag="m16")
             vc = prep3.tile([P, HKV * D], U32, tag="vc", align_bytes=64)
             vs = prep3.tile([P, HKV * D], U8, tag="vs", align_bytes=64)
-            ready[b] = (qT, kT, m16, vc, vs)
+            ready[b] = (qT, kT, vc, vs)
 
-        def prep_words(src, dst, blk):
+        def prep_words(src, dst, blk, on_vector):
             tq = ps_tq.tile([P, NT, P], F32, tag="tq")
             for t in range(NT):
                 c0 = (blk * NT + t) * W
                 nc.tensor.transpose(tq[:, t, :], src[:].bitcast(F32)[:, c0 : c0 + W], ident_f[:])
-            nc.scalar.copy(out=dst[:, blk * NT * P : (blk + 1) * NT * P], in_=tq[:].rearrange("p t q -> p (t q)"))
+            if on_vector:
+                nc.vector.tensor_copy(
+                    out=dst[:, blk * NT * P : (blk + 1) * NT * P], in_=tq[:].rearrange("p t q -> p (t q)")
+                )
+            else:
+                nc.scalar.copy(out=dst[:, blk * NT * P : (blk + 1) * NT * P], in_=tq[:].rearrange("p t q -> p (t q)"))
 
         def prep_mask_value(b):
             q_sb, k_sb, v_sb, m_sb = loaded[b]
-            qT, kT, m16, vc, vs = ready[b]
-            nc.gpsimd.tensor_scalar(out=m16[:], in0=m_sb[:], scalar1=16.0, scalar2=0.0, op0=ALU.mult, op1=ALU.add)
+            qT, kT, vc, vs = ready[b]
             vg = prep.tile([P, HKV * D * NT], BF16, tag="vg", align_bytes=64)
-            nc.vector.tensor_copy(
-                out=vg[:].rearrange("p (g d t) -> p g d t", g=HKV, t=NT),
-                in_=v_sb[:].rearrange("p (g t d) -> p g d t", g=HKV, t=NT),
-            )
+            for g in range(HKV):
+                nc.vector.tensor_copy(
+                    out=vg[:, g * D * NT : (g + 1) * D * NT].rearrange("p (c i t) -> p c t i", i=4, t=NT),
+                    in_=v_sb[:, g * D * NT : (g + 1) * D * NT].rearrange("p (t c i) -> p c t i", i=4, t=NT),
+                )
             nc.vector.quantize_mx(out=vc[:].bitcast(FP8X4), scales=vs[:], in_=vg[:])
 
         def prep_chunk(b, j):
@@ -105,21 +112,21 @@ def tile_deepseekv4attention_t_kernel(tc, query, key, value, attention_mask, sin
             if j == 0:
                 prep_alloc(b)
             q_sb, k_sb, v_sb, m_sb = loaded[b]
-            qT, kT, m16, vc, vs = ready[b]
+            qT, kT, vc, vs = ready[b]
             if j == 0:
-                prep_words(k_sb, kT, 0)
+                prep_words(k_sb, kT, 0, False)
             elif j == 1:
-                prep_words(q_sb, qT, 0)
+                prep_words(q_sb, qT, 0, True)
             elif j == 2:
-                prep_words(q_sb, qT, 1)
+                prep_words(q_sb, qT, 1, False)
             elif j == 3:
-                prep_words(k_sb, kT, 1)
+                prep_words(k_sb, kT, 1, True)
             elif j == 4:
                 prep_mask_value(b)
             elif j == 5:
-                prep_words(q_sb, qT, 2)
+                prep_words(q_sb, qT, 2, False)
             elif j == 6:
-                prep_words(q_sb, qT, 3)
+                prep_words(q_sb, qT, 3, True)
 
         st = {}
 
@@ -131,10 +138,11 @@ def tile_deepseekv4attention_t_kernel(tc, query, key, value, attention_mask, sin
         def stage_a(n):
             b, tp, h = where(n)
             g = h // G
-            qT, kT, m16, vc, vs = ready[b]
+            qT, kT, vc, vs = ready[b]
             qTb = qT[:].bitcast(BF16).rearrange("p (c e) -> p c e", e=2)
             kTb = kT[:].bitcast(BF16).rearrange("p (c e) -> p c e", e=2)
-            s16 = work.tile([P, 2, S], F32, tag="s16")
+            m_sb = loaded[b][3]
+            s_h = s_bufs[h]
             for i in range(2):
                 t = 2 * tp + i
                 sc = ps_sc.tile([P, S], F32, tag="sc")
@@ -147,34 +155,33 @@ def tile_deepseekv4attention_t_kernel(tc, query, key, value, attention_mask, sin
                         start=(e == 0),
                         stop=(e == 1),
                     )
-                nc.vector.tensor_tensor(out=s16[:, i, :], in0=sc[:], in1=m16[:, t * S : (t + 1) * S], op=ALU.add)
-            mx = stat.tile([P, 2], F32, tag="mx")
-            nc.vector.tensor_reduce(out=mx[:], in_=s16[:], axis=AX.X, op=ALU.max)
+                nc.vector.scalar_tensor_tensor(
+                    out=s_h[:, i, 0:S],
+                    in0=sc[:],
+                    scalar=1.0 / 16.0,
+                    in1=m_sb[:, t * S : (t + 1) * S],
+                    op0=ALU.mult,
+                    op1=ALU.add,
+                )
             negm = stat.tile([P, 2], F32, tag="negm")
-            nc.vector.tensor_scalar(
-                out=negm[:], in0=mx[:], scalar1=sink16[:, h : h + 1], scalar2=-1.0 / 16.0, op0=ALU.max, op1=ALU.mult
-            )
-            st[n] = {"s16": s16, "negm": negm}
+            nc.vector.tensor_reduce(out=negm[:], in_=s_h[:, :, 0 : S + 1], axis=AX.X, op=ALU.max, negate=True)
+            st[n] = {"negm": negm}
 
         def stage_b(n):
             b, tp, h = where(n)
-            s16 = st[n]["s16"]
+            s_h = s_bufs[h]
             negm = st[n]["negm"]
-            e_sb = work.tile([P, 2, S], BF16, tag="e_sb")
-            rsum = stat.tile([P, 2], F32, tag="rsum")
+            e_sb = work.tile([P, 2, SW], BF16, tag="e_sb")
+            den = stat.tile([P, 2], F32, tag="den")
             for i in range(2):
                 nc.scalar.activation(
-                    out=e_sb[:, i, :],
-                    in_=s16[:, i, :],
+                    out=e_sb[:, i, 0 : S + 1],
+                    in_=s_h[:, i, 0 : S + 1],
                     func=ACT.Exp,
                     bias=negm[:, i : i + 1],
-                    scale=1.0 / 16.0,
-                    accum_out=rsum[:, i : i + 1],
+                    scale=1.0,
+                    accum_out=den[:, i : i + 1],
                 )
-            sterm = stat.tile([P, 2], F32, tag="sterm")
-            nc.scalar.activation(out=sterm[:], in_=negm[:], func=ACT.Exp, bias=sink_f[:, h : h + 1], scale=1.0)
-            den = stat.tile([P, 2], F32, tag="den")
-            nc.vector.tensor_tensor(out=den[:], in0=rsum[:], in1=sterm[:], op=ALU.add)
             rden = stat.tile([P, 2], F32, tag="rden")
             nc.vector.reciprocal(out=rden[:], in_=den[:])
             et = ps_et.tile([P, 2, NT, P], BF16, tag="et")
@@ -202,7 +209,7 @@ def tile_deepseekv4attention_t_kernel(tc, query, key, value, attention_mask, sin
         def stage_d(n):
             b, tp, h = where(n)
             g = h // G
-            qT, kT, m16, vc, vs = ready[b]
+            qT, kT, vc, vs = ready[b]
             ec = st[n]["ec"]
             es = st[n]["es"]
             rden = st[n]["rden"]
@@ -231,13 +238,14 @@ def tile_deepseekv4attention_t_kernel(tc, query, key, value, attention_mask, sin
 
         load(0)
         load(1)
-        for j in range(DUOS_PER_BATCH):
-            prep_chunk(0, j)
+        first = {0: (0, 1), 1: (2,), 2: (3, 5, 4), 3: (6,)}
         for n in range(N_DUOS + 3):
             b, j = divmod(n, DUOS_PER_BATCH)
             if n < N_DUOS:
                 if j == 0 and b + 2 < B:
                     load(b + 2)
+                for c in first.get(n, ()):
+                    prep_chunk(0, c)
                 stage_a(n)
                 prep_chunk(b + 1, j)
             if 0 <= n - 1 < N_DUOS:

@@ -1,8 +1,6 @@
 from contextlib import ExitStack
 
-import concourse.bass as bass
 import concourse.mybir as mybir
-import concourse.tile as tile
 from concourse.masks import make_identity
 
 F32 = mybir.dt.float32
@@ -23,6 +21,7 @@ SW = 520
 FLOPS = 2 * 2 * B * H * S * S * D
 DUOS_PER_BATCH = H * NT // 2
 N_DUOS = B * DUOS_PER_BATCH
+CHUNKS = (("k", 0), ("q", 0), ("q", 1), ("k", 1), ("q", 2), ("q", 3))
 
 
 def tile_deepseekv4attention_t_kernel(tc, query, key, value, attention_mask, sinks, out):
@@ -33,186 +32,225 @@ def tile_deepseekv4attention_t_kernel(tc, query, key, value, attention_mask, sin
         prep = ctx.enter_context(tc.tile_pool(name="prep", bufs=2))
         prep3 = ctx.enter_context(tc.tile_pool(name="prep3", bufs=3))
         work = ctx.enter_context(tc.tile_pool(name="work", bufs=3))
+        one = ctx.enter_context(tc.tile_pool(name="one", bufs=1))
         stat = ctx.enter_context(tc.tile_pool(name="stat", bufs=6))
         outp = ctx.enter_context(tc.tile_pool(name="outp", bufs=3))
         ps_sc = ctx.enter_context(tc.psum_pool(name="ps_sc", bufs=3))
         ps_et = ctx.enter_context(tc.psum_pool(name="ps_et", bufs=2))
         ps_o = ctx.enter_context(tc.psum_pool(name="ps_o", bufs=2))
         ps_tq = ctx.enter_context(tc.psum_pool(name="ps_tq", bufs=1))
-
-        ident_f = const.tile([P, P], F32)
-        make_identity(nc, ident_f[:])
-        ident_b = const.tile([P, P], BF16)
-        make_identity(nc, ident_b[:])
-        sink_raw = const.tile([P, H], BF16)
-        nc.sync.dma_start(out=sink_raw[:], in_=sinks.partition_broadcast(P))
-        s_bufs = []
-        for h in range(H):
-            s_h = const.tile([P, 2, SW], F32, name="s_h%d" % h)
-            for i in range(2):
-                nc.vector.tensor_copy(out=s_h[:, i, S : S + 1], in_=sink_raw[:, h : h + 1])
-            s_bufs.append(s_h)
+        ctx.enter_context(tc.manual_schedule())
 
         loaded = {}
         ready = {}
-
-        def load(b):
-            k_sb = ld.tile([P, HKV * NT * D], BF16, tag="k_sb")
-            nc.sync.dma_start(
-                out=k_sb[:].rearrange("p (x d) -> p x d", d=D),
-                in_=key[b].rearrange("g (t p) d -> p (g t) d", p=P),
-            )
-            q_sb = ld.tile([P, H * NT * D], BF16, tag="q_sb")
-            nc.sync.dma_start(
-                out=q_sb[:].rearrange("p (h x) -> p h x", h=H),
-                in_=query[b].rearrange("h (p t) d -> p h (t d)", t=NT),
-            )
-            m_sb = ld.tile([P, NT * S], BF16, tag="m_sb")
-            nc.sync.dma_start(out=m_sb[:], in_=attention_mask[b, 0].rearrange("(p t) k -> p (t k)", t=NT))
-            v_sb = ld.tile([P, HKV * NT * D], BF16, tag="v_sb")
-            nc.sync.dma_start(
-                out=v_sb[:].rearrange("p (x d) -> p x d", d=D),
-                in_=value[b].rearrange("g (t p) d -> p (g t) d", p=P),
-            )
-            loaded[b] = (q_sb, k_sb, v_sb, m_sb)
-
-        def prep_alloc(b):
-            qT = prep.tile([P, H * NT * P], F32, tag="qT")
-            kT = prep.tile([P, HKV * NT * P], F32, tag="kT")
-            vc = prep3.tile([P, HKV * D], U32, tag="vc", align_bytes=64)
-            vs = prep3.tile([P, HKV * D], U8, tag="vs", align_bytes=64)
-            ready[b] = (qT, kT, vc, vs)
-
-        def prep_words(src, dst, blk, on_vector):
-            tq = ps_tq.tile([P, NT, P], F32, tag="tq")
-            for t in range(NT):
-                c0 = (blk * NT + t) * W
-                nc.tensor.transpose(tq[:, t, :], src[:].bitcast(F32)[:, c0 : c0 + W], ident_f[:])
-            if on_vector:
-                nc.vector.tensor_copy(
-                    out=dst[:, blk * NT * P : (blk + 1) * NT * P], in_=tq[:].rearrange("p t q -> p (t q)")
-                )
-            else:
-                nc.scalar.copy(out=dst[:, blk * NT * P : (blk + 1) * NT * P], in_=tq[:].rearrange("p t q -> p (t q)"))
-
-        def prep_mask_value(b):
-            q_sb, k_sb, v_sb, m_sb = loaded[b]
-            qT, kT, vc, vs = ready[b]
-            vg = prep.tile([P, HKV * D * NT], BF16, tag="vg", align_bytes=64)
-            for g in range(HKV):
-                nc.vector.tensor_copy(
-                    out=vg[:, g * D * NT : (g + 1) * D * NT].rearrange("p (c i t) -> p c t i", i=4, t=NT),
-                    in_=v_sb[:, g * D * NT : (g + 1) * D * NT].rearrange("p (t c i) -> p c t i", i=4, t=NT),
-                )
-            nc.vector.quantize_mx(out=vc[:].bitcast(FP8X4), scales=vs[:], in_=vg[:])
-
-        def prep_chunk(b, j):
-            if b >= B:
-                return
-            if j == 0:
-                prep_alloc(b)
-            q_sb, k_sb, v_sb, m_sb = loaded[b]
-            qT, kT, vc, vs = ready[b]
-            if j == 0:
-                prep_words(k_sb, kT, 0, False)
-            elif j == 1:
-                prep_words(q_sb, qT, 0, True)
-            elif j == 2:
-                prep_words(q_sb, qT, 1, False)
-            elif j == 3:
-                prep_words(k_sb, kT, 1, True)
-            elif j == 4:
-                prep_mask_value(b)
-            elif j == 5:
-                prep_words(q_sb, qT, 2, False)
-            elif j == 6:
-                prep_words(q_sb, qT, 3, True)
-
         st = {}
+        osb = {}
+
+        def valid(n):
+            return 0 <= n < N_DUOS
 
         def where(n):
             b, j = divmod(n, DUOS_PER_BATCH)
             tp, h = divmod(j, H)
             return b, tp, h
 
-        def stage_a(n):
+        def load(b, fine):
+            k_sb = ld.tile([P, HKV * NT * D], BF16, tag="k_sb")
+            q_sb = ld.tile([P, H * NT * D], BF16, tag="q_sb")
+            m_sb = ld.tile([P, NT * S], BF16, tag="m_sb")
+            v_sb = ld.tile([P, HKV * NT * D], BF16, tag="v_sb")
+            loaded[b] = {"q": q_sb, "k": k_sb, "v": v_sb, "m": m_sb}
+            blk = NT * D
+
+            def load_k(g0, g1):
+                nc.sync.dma_start(
+                    out=k_sb[:, g0 * blk : g1 * blk].rearrange("p (x d) -> p x d", d=D),
+                    in_=key[b, g0:g1].rearrange("g (t p) d -> p (g t) d", p=P),
+                )
+
+            def load_q(h0, h1):
+                nc.sync.dma_start(
+                    out=q_sb[:, h0 * blk : h1 * blk].rearrange("p (h x) -> p h x", x=blk),
+                    in_=query[b, h0:h1].rearrange("h (p t) d -> p h (t d)", t=NT),
+                )
+
+            def load_m():
+                nc.sync.dma_start(out=m_sb[:], in_=attention_mask[b, 0].rearrange("(p t) k -> p (t k)", t=NT))
+
+            if fine:
+                load_k(0, 1)
+                load_q(0, 1)
+                load_m()
+                load_q(1, 2)
+                load_k(1, 2)
+                load_q(2, 4)
+            else:
+                load_k(0, HKV)
+                load_q(0, H)
+                load_m()
+            nc.sync.dma_start(
+                out=v_sb[:].rearrange("p (x d) -> p x d", d=D),
+                in_=value[b].rearrange("g (t p) d -> p (g t) d", p=P),
+            )
+
+        def prep_alloc(b):
+            qT = prep.tile([P, H * NT * P], F32, tag="qT")
+            kT = prep.tile([P, HKV * NT * P], F32, tag="kT")
+            vg = prep.tile([P, HKV * D * NT], BF16, tag="vg", align_bytes=64)
+            vc = prep3.tile([P, HKV * D], U32, tag="vc", align_bytes=64)
+            vs = prep3.tile([P, HKV * D], U8, tag="vs", align_bytes=64)
+            ready[b] = {"q": qT, "k": kT, "vg": vg, "vc": vc, "vs": vs}
+
+        def words(b, c, on_vector):
+            if b >= B:
+                return
+            if c == 0:
+                prep_alloc(b)
+            which, blk = CHUNKS[c]
+            src = loaded[b][which]
+            dst = ready[b][which]
+            tq = ps_tq.tile([P, NT, P], F32, tag="tq")
+            for t in range(NT):
+                c0 = (blk * NT + t) * W
+                nc.tensor.transpose(tq[:, t, :], src[:].bitcast(F32)[:, c0 : c0 + W], ident_f[:])
+            dst_cols = dst[:, blk * NT * P : (blk + 1) * NT * P]
+            if on_vector:
+                nc.vector.tensor_copy(out=dst_cols, in_=tq[:].rearrange("p t q -> p (t q)"))
+            else:
+                nc.scalar.copy(out=dst_cols, in_=tq[:].rearrange("p t q -> p (t q)"))
+
+        def value_group(b, g):
+            if b >= B:
+                return
+            v_sb = loaded[b]["v"]
+            vg = ready[b]["vg"]
+            nc.vector.tensor_copy(
+                out=vg[:, g * D * NT : (g + 1) * D * NT].rearrange("p (c i t) -> p c t i", i=4, t=NT),
+                in_=v_sb[:, g * D * NT : (g + 1) * D * NT].rearrange("p (t c i) -> p c t i", i=4, t=NT),
+            )
+
+        def value_quant(b):
+            if b >= B:
+                return
+            r = ready[b]
+            nc.vector.quantize_mx(out=r["vc"][:].bitcast(FP8X4), scales=r["vs"][:], in_=r["vg"][:])
+
+        def qk(n, i):
+            if not valid(n):
+                return
             b, tp, h = where(n)
             g = h // G
-            qT, kT, vc, vs = ready[b]
-            qTb = qT[:].bitcast(BF16).rearrange("p (c e) -> p c e", e=2)
-            kTb = kT[:].bitcast(BF16).rearrange("p (c e) -> p c e", e=2)
-            m_sb = loaded[b][3]
-            s_h = s_bufs[h]
-            for i in range(2):
-                t = 2 * tp + i
-                sc = ps_sc.tile([P, S], F32, tag="sc")
-                c0 = (h * NT + t) * P
-                for e in range(2):
-                    nc.tensor.matmul(
-                        sc[:],
-                        lhsT=qTb[:, c0 : c0 + P, e],
-                        rhs=kTb[:, g * S : (g + 1) * S, e],
-                        start=(e == 0),
-                        stop=(e == 1),
-                    )
-                nc.vector.scalar_tensor_tensor(
-                    out=s_h[:, i, 0:S],
-                    in0=sc[:],
-                    scalar=1.0 / 16.0,
-                    in1=m_sb[:, t * S : (t + 1) * S],
-                    op0=ALU.mult,
-                    op1=ALU.add,
+            qTb = ready[b]["q"][:].bitcast(BF16).rearrange("p (c e) -> p c e", e=2)
+            kTb = ready[b]["k"][:].bitcast(BF16).rearrange("p (c e) -> p c e", e=2)
+            sc = ps_sc.tile([P, S], F32, tag="sc")
+            c0 = (h * NT + 2 * tp + i) * P
+            for e in range(2):
+                nc.tensor.matmul(
+                    sc[:],
+                    lhsT=qTb[:, c0 : c0 + P, e],
+                    rhs=kTb[:, g * S : (g + 1) * S, e],
+                    start=(e == 0),
+                    stop=(e == 1),
                 )
-            negm = stat.tile([P, 2], F32, tag="negm")
-            nc.vector.tensor_reduce(out=negm[:], in_=s_h[:, :, 0 : S + 1], axis=AX.X, op=ALU.max, negate=True)
-            st[n] = {"negm": negm}
+            st[(n, "sc", i)] = sc
 
-        def stage_b(n):
+        def add_mask(n, i):
+            if not valid(n):
+                return
             b, tp, h = where(n)
-            s_h = s_bufs[h]
-            negm = st[n]["negm"]
+            t = 2 * tp + i
+            nc.vector.scalar_tensor_tensor(
+                out=s_bufs[h][:, i, 0:S],
+                in0=st[(n, "sc", i)][:],
+                scalar=1.0 / 16.0,
+                in1=loaded[b]["m"][:, t * S : (t + 1) * S],
+                op0=ALU.mult,
+                op1=ALU.add,
+            )
+
+        def row_max(n):
+            if not valid(n):
+                return
+            b, tp, h = where(n)
+            negm = stat.tile([P, 2], F32, tag="negm")
+            nc.vector.tensor_reduce(out=negm[:], in_=s_bufs[h][:, :, 0 : S + 1], axis=AX.X, op=ALU.max, negate=True)
+            st[(n, "negm")] = negm
+
+        def exps(n):
+            if not valid(n):
+                return
+            b, tp, h = where(n)
+            negm = st[(n, "negm")]
             e_sb = work.tile([P, 2, SW], BF16, tag="e_sb")
             den = stat.tile([P, 2], F32, tag="den")
             for i in range(2):
                 nc.scalar.activation(
                     out=e_sb[:, i, 0 : S + 1],
-                    in_=s_h[:, i, 0 : S + 1],
+                    in_=s_bufs[h][:, i, 0 : S + 1],
                     func=ACT.Exp,
                     bias=negm[:, i : i + 1],
                     scale=1.0,
                     accum_out=den[:, i : i + 1],
                 )
+            st[(n, "e")] = e_sb
+            st[(n, "den")] = den
+
+        def recip(n):
+            if not valid(n):
+                return
             rden = stat.tile([P, 2], F32, tag="rden")
-            nc.vector.reciprocal(out=rden[:], in_=den[:])
+            nc.vector.reciprocal(out=rden[:], in_=st[(n, "den")][:])
+            st[(n, "rden")] = rden
+
+        def e_transposes(n):
+            if not valid(n):
+                return
+            e_sb = st[(n, "e")]
             et = ps_et.tile([P, 2, NT, P], BF16, tag="et")
             for i in range(2):
                 for k in range(NT):
                     nc.tensor.transpose(et[:, i, k, :], e_sb[:, i, k * P : (k + 1) * P], ident_b[:])
-            st[n]["et"] = et
-            st[n]["rden"] = rden
+            st[(n, "et")] = et
 
-        def stage_c(n):
-            et = st[n]["et"]
-            gr = work.tile([P, 2 * P * NT], BF16, tag="gr", align_bytes=64)
-            nc.scalar.copy(
+        def e_out_of_psum(n):
+            if not valid(n):
+                return
+            etc = work.tile([P, 2 * NT * P], BF16, tag="etc")
+            nc.scalar.copy(out=etc[:], in_=st[(n, "et")][:].rearrange("p i k q -> p (i k q)"))
+            st[(n, "etc")] = etc
+
+        def e_regroup(n):
+            if not valid(n):
+                return
+            gr = one.tile([P, 2 * P * NT], BF16, tag="gr", align_bytes=64)
+            nc.gpsimd.tensor_scalar(
                 out=gr[:].rearrange("p (i q k) -> p i q k", i=2, k=NT),
-                in_=et[:].rearrange("p i k q -> p i q k"),
+                in0=st[(n, "etc")][:].rearrange("p (i k q) -> p i q k", i=2, k=NT),
+                scalar1=1.0,
+                scalar2=0.0,
+                op0=ALU.mult,
+                op1=ALU.add,
             )
+            st[(n, "gr")] = gr
+
+        def e_quant(n):
+            if not valid(n):
+                return
             ec = work.tile([P, 2 * P], U32, tag="ec", align_bytes=64)
             es = work.tile([P, 2 * P], U8, tag="es", align_bytes=64)
-            nc.vector.quantize_mx(out=ec[:].bitcast(FP8X4), scales=es[:], in_=gr[:])
-            st[n]["ec"] = ec
-            st[n]["es"] = es
+            nc.vector.quantize_mx(out=ec[:].bitcast(FP8X4), scales=es[:], in_=st[(n, "gr")][:])
+            st[(n, "ec")] = ec
+            st[(n, "es")] = es
 
-        osb = {}
-
-        def stage_d(n):
+        def pv(n):
+            if not valid(n):
+                return
             b, tp, h = where(n)
             g = h // G
-            qT, kT, vc, vs = ready[b]
-            ec = st[n]["ec"]
-            es = st[n]["es"]
-            rden = st[n]["rden"]
+            vc = ready[b]["vc"]
+            vs = ready[b]["vs"]
+            ec = st[(n, "ec")]
+            es = st[(n, "es")]
             o_ps = ps_o.tile([P, 2, D], F32, tag="o_ps")
             for i in range(2):
                 nc.tensor.matmul_mx(
@@ -224,9 +262,17 @@ def tile_deepseekv4attention_t_kernel(tc, query, key, value, attention_mask, sin
                     start=True,
                     stop=True,
                 )
+            st[(n, "o")] = o_ps
+
+        def finish(n):
+            if not valid(n):
+                return
+            b, tp, h = where(n)
+            o_ps = st[(n, "o")]
+            rden = st[(n, "rden")]
             if h == 0:
-                o_sb = outp.tile([P, 2, H, D], F32, tag="o_sb")
-                osb[(b, tp)] = o_sb
+                o_new = outp.tile([P, 2, H, D], F32, tag="o_sb")
+                osb[(b, tp)] = o_new
             o_sb = osb[(b, tp)]
             for i in range(2):
                 nc.scalar.activation(out=o_sb[:, i, h, :], in_=o_ps[:, i, :], func=ACT.Copy, scale=rden[:, i : i + 1])
@@ -236,21 +282,51 @@ def tile_deepseekv4attention_t_kernel(tc, query, key, value, attention_mask, sin
                     in_=o_sb[:].rearrange("p i h d -> p i (h d)"),
                 )
 
-        load(0)
-        load(1)
-        first = {0: (0, 1), 1: (2,), 2: (3, 5, 4), 3: (6,)}
-        for n in range(N_DUOS + 3):
-            b, j = divmod(n, DUOS_PER_BATCH)
-            if n < N_DUOS:
-                if j == 0 and b + 2 < B:
-                    load(b + 2)
-                for c in first.get(n, ()):
-                    prep_chunk(0, c)
-                stage_a(n)
-                prep_chunk(b + 1, j)
-            if 0 <= n - 1 < N_DUOS:
-                stage_b(n - 1)
-            if 0 <= n - 2 < N_DUOS:
-                stage_c(n - 2)
-            if 0 <= n - 3 < N_DUOS:
-                stage_d(n - 3)
+        sink_raw = const.tile([P, H], BF16)
+        nc.scalar.dma_start(out=sink_raw[:], in_=sinks.partition_broadcast(P))
+        load(0, True)
+        load(1, False)
+        ident_f = const.tile([P, P], F32)
+        make_identity(nc, ident_f[:])
+        ident_b = const.tile([P, P], BF16)
+        make_identity(nc, ident_b[:])
+        s_bufs = []
+        for h in range(H):
+            s_h = const.tile([P, 2, SW], F32, name="s_h%d" % h)
+            for i in range(2):
+                nc.vector.tensor_copy(out=s_h[:, i, S : S + 1], in_=sink_raw[:, h : h + 1])
+            s_bufs.append(s_h)
+
+        words(0, 0, False)
+        words(0, 1, True)
+        early = {-1: (2,), 0: (3, 4), 1: (5,)}
+        for m in range(-1, N_DUOS + 3):
+            b, j = divmod(m, DUOS_PER_BATCH)
+            if valid(m) and j == 0 and b + 2 < B:
+                load(b + 2, False)
+            exps(m - 1)
+            add_mask(m, 0)
+            add_mask(m, 1)
+            e_transposes(m - 1)
+            finish(m - 3)
+            if m == 1:
+                value_group(0, 0)
+                value_group(0, 1)
+                value_quant(0)
+            if valid(m) and j == 2:
+                value_group(b + 1, 0)
+            if valid(m) and j == 3:
+                value_group(b + 1, 1)
+                value_quant(b + 1)
+            e_quant(m - 2)
+            qk(m + 1, 0)
+            pv(m - 2)
+            qk(m + 1, 1)
+            e_out_of_psum(m - 1)
+            e_regroup(m - 1)
+            row_max(m)
+            recip(m - 1)
+            for c in early.get(m, ()):
+                words(0, c, c % 2 == 1)
+            if valid(m) and j < len(CHUNKS):
+                words(b + 1, j, False)

@@ -37,8 +37,8 @@ def tile_deepseekv4attention_t_kernel(tc, query, key, value, attention_mask, sin
         outp = ctx.enter_context(tc.tile_pool(name="outp", bufs=3))
         ps_sc = ctx.enter_context(tc.psum_pool(name="ps_sc", bufs=3))
         ps_et = ctx.enter_context(tc.psum_pool(name="ps_et", bufs=2))
-        ps_o = ctx.enter_context(tc.psum_pool(name="ps_o", bufs=2))
-        ps_tq = ctx.enter_context(tc.psum_pool(name="ps_tq", bufs=1))
+        ps_o = ctx.enter_context(tc.psum_pool(name="ps_o", bufs=1))
+        ps_tq = ctx.enter_context(tc.psum_pool(name="ps_tq", bufs=2))
         ctx.enter_context(tc.manual_schedule())
 
         loaded = {}
@@ -101,18 +101,23 @@ def tile_deepseekv4attention_t_kernel(tc, query, key, value, attention_mask, sin
             vs = prep3.tile([P, HKV * D], U8, tag="vs", align_bytes=64)
             ready[b] = {"q": qT, "k": kT, "vg": vg, "vc": vc, "vs": vs}
 
-        def words(b, c, on_vector):
-            if b >= B:
+        def words_transpose(b, c):
+            if b >= B or not 0 <= c < len(CHUNKS):
                 return
-            if c == 0:
-                prep_alloc(b)
             which, blk = CHUNKS[c]
             src = loaded[b][which]
-            dst = ready[b][which]
             tq = ps_tq.tile([P, NT, P], F32, tag="tq")
             for t in range(NT):
                 c0 = (blk * NT + t) * W
                 nc.tensor.transpose(tq[:, t, :], src[:].bitcast(F32)[:, c0 : c0 + W], ident_f[:])
+            st[(b, "tq", c)] = tq
+
+        def words_copy(b, c, on_vector):
+            if b >= B or not 0 <= c < len(CHUNKS):
+                return
+            which, blk = CHUNKS[c]
+            dst = ready[b][which]
+            tq = st[(b, "tq", c)]
             dst_cols = dst[:, blk * NT * P : (blk + 1) * NT * P]
             if on_vector:
                 nc.vector.tensor_copy(out=dst_cols, in_=tq[:].rearrange("p t q -> p (t q)"))
@@ -297,18 +302,27 @@ def tile_deepseekv4attention_t_kernel(tc, query, key, value, attention_mask, sin
                 nc.vector.tensor_copy(out=s_h[:, i, S : S + 1], in_=sink_raw[:, h : h + 1])
             s_bufs.append(s_h)
 
-        words(0, 0, False)
-        words(0, 1, True)
-        early = {-1: (2,), 0: (3, 4), 1: (5,)}
-        for m in range(-1, N_DUOS + 3):
+        first_need = {0: (0, 1), 1: (2,), 2: (3, 4), 3: (5,)}
+        prep_alloc(0)
+        for m in range(-1, N_DUOS + 4):
             b, j = divmod(m, DUOS_PER_BATCH)
             if valid(m) and j == 0 and b + 2 < B:
                 load(b + 2, False)
+            if valid(m) and j == 0 and b + 1 < B:
+                prep_alloc(b + 1)
             exps(m - 1)
             add_mask(m, 0)
             add_mask(m, 1)
+            for c in first_need.get(m + 1, ()):
+                words_transpose(0, c)
+                words_copy(0, c, c % 2 == 1)
+            qk(m + 1, 0)
+            pv(m - 4)
+            qk(m + 1, 1)
+            e_out_of_psum(m - 2)
             e_transposes(m - 1)
-            finish(m - 3)
+            finish(m - 4)
+            row_max(m)
             if m == 1:
                 value_group(0, 0)
                 value_group(0, 1)
@@ -317,16 +331,13 @@ def tile_deepseekv4attention_t_kernel(tc, query, key, value, attention_mask, sin
                 value_group(b + 1, 0)
             if valid(m) and j == 3:
                 value_group(b + 1, 1)
+            if valid(m) and j == 4:
                 value_quant(b + 1)
-            e_quant(m - 2)
-            qk(m + 1, 0)
-            pv(m - 2)
-            qk(m + 1, 1)
-            e_out_of_psum(m - 1)
-            e_regroup(m - 1)
-            row_max(m)
-            recip(m - 1)
-            for c in early.get(m, ()):
-                words(0, c, c % 2 == 1)
-            if valid(m) and j < len(CHUNKS):
-                words(b + 1, j, False)
+            e_quant(m - 3)
+            recip(m - 2)
+            e_regroup(m - 2)
+            if valid(m - 1):
+                b1, j1 = divmod(m - 1, DUOS_PER_BATCH)
+                words_copy(b1 + 1, j1 - 2, False)
+            if valid(m):
+                words_transpose(b + 1, j - 2)

@@ -74,20 +74,25 @@ def tile_deepseekv4attention_t_kernel(tc, query, key, value, attention_mask, sin
                     in_=query[b, h0:h1].rearrange("h (p t) d -> p h (t d)", t=NT),
                 )
 
-            def load_m():
-                nc.sync.dma_start(out=m_sb[:], in_=attention_mask[b, 0].rearrange("(p t) k -> p (t k)", t=NT))
+            def load_m(t0, t1):
+                nc.sync.dma_start(
+                    out=m_sb[:, t0 * S : t1 * S],
+                    in_=attention_mask[b, 0].rearrange("(p t) k -> p t k", t=NT)[:, t0:t1, :].rearrange("p t k -> p (t k)"),
+                )
 
             if fine:
                 load_k(0, 1)
                 load_q(0, 1)
-                load_m()
+                load_m(0, 2)
                 load_q(1, 2)
                 load_k(1, 2)
-                load_q(2, 4)
+                load_q(2, 3)
+                load_q(3, 4)
+                load_m(2, NT)
             else:
                 load_k(0, HKV)
                 load_q(0, H)
-                load_m()
+                load_m(0, NT)
             nc.sync.dma_start(
                 out=v_sb[:].rearrange("p (x d) -> p x d", d=D),
                 in_=value[b].rearrange("g (t p) d -> p (g t) d", p=P),
@@ -220,17 +225,21 @@ def tile_deepseekv4attention_t_kernel(tc, query, key, value, attention_mask, sin
         def e_out_of_psum(n):
             if not valid(n):
                 return
-            etc = work.tile([P, 2 * NT * P], BF16, tag="etc")
-            nc.scalar.copy(out=etc[:], in_=st[(n, "et")][:].rearrange("p i k q -> p (i k q)"))
+            et = st[(n, "et")]
+            etc = work.tile([P, NT * P], BF16, tag="etc")
+            nc.scalar.copy(out=etc[:], in_=et[:, 1].rearrange("p k q -> p (k q)"))
             st[(n, "etc")] = etc
+            gr_a = work.tile([P, P * NT], BF16, tag="gr_a", align_bytes=64)
+            nc.scalar.copy(out=gr_a[:].rearrange("p (q k) -> p q k", k=NT), in_=et[:, 0].rearrange("p k q -> p q k"))
+            st[(n, "gr_a")] = gr_a
 
         def e_regroup(n):
             if not valid(n):
                 return
-            gr = one.tile([P, 2 * P * NT], BF16, tag="gr", align_bytes=64)
+            gr = one.tile([P, P * NT], BF16, tag="gr", align_bytes=64)
             nc.gpsimd.tensor_scalar(
-                out=gr[:].rearrange("p (i q k) -> p i q k", i=2, k=NT),
-                in0=st[(n, "etc")][:].rearrange("p (i k q) -> p i q k", i=2, k=NT),
+                out=gr[:].rearrange("p (q k) -> p q k", k=NT),
+                in0=st[(n, "etc")][:].rearrange("p (k q) -> p q k", k=NT),
                 scalar1=1.0,
                 scalar2=0.0,
                 op0=ALU.mult,
@@ -243,7 +252,8 @@ def tile_deepseekv4attention_t_kernel(tc, query, key, value, attention_mask, sin
                 return
             ec = work.tile([P, 2 * P], U32, tag="ec", align_bytes=64)
             es = work.tile([P, 2 * P], U8, tag="es", align_bytes=64)
-            nc.vector.quantize_mx(out=ec[:].bitcast(FP8X4), scales=es[:], in_=st[(n, "gr")][:])
+            nc.vector.quantize_mx(out=ec[:, 0:P].bitcast(FP8X4), scales=es[:, 0:P], in_=st[(n, "gr_a")][:])
+            nc.vector.quantize_mx(out=ec[:, P : 2 * P].bitcast(FP8X4), scales=es[:, P : 2 * P], in_=st[(n, "gr")][:])
             st[(n, "ec")] = ec
             st[(n, "es")] = es
 
@@ -281,7 +291,12 @@ def tile_deepseekv4attention_t_kernel(tc, query, key, value, attention_mask, sin
             o_sb = osb[(b, tp)]
             for i in range(2):
                 nc.scalar.activation(out=o_sb[:, i, h, :], in_=o_ps[:, i, :], func=ACT.Copy, scale=rden[:, i : i + 1])
-            if h == H - 1:
+            if b == B - 1 and tp == 1:
+                nc.sync.dma_start(
+                    out=out[b].rearrange("(p t) h d -> p t h d", t=NT)[:, 2 * tp : 2 * tp + 2, h, :],
+                    in_=o_sb[:, :, h, :],
+                )
+            elif h == H - 1:
                 nc.sync.dma_start(
                     out=out[b].rearrange("(p t) h d -> p t (h d)", t=NT)[:, 2 * tp : 2 * tp + 2, :],
                     in_=o_sb[:].rearrange("p i h d -> p i (h d)"),
@@ -338,6 +353,6 @@ def tile_deepseekv4attention_t_kernel(tc, query, key, value, attention_mask, sin
             e_regroup(m - 2)
             if valid(m - 1):
                 b1, j1 = divmod(m - 1, DUOS_PER_BATCH)
-                words_copy(b1 + 1, j1 - 2, False)
+                words_copy(b1 + 1, j1 - 2, j1 - 2 == 0)
             if valid(m):
                 words_transpose(b + 1, j - 2)

@@ -18,6 +18,8 @@ P = 128
 NT = S // P
 W = D // 2
 SW = 520
+DEN_STEP = 8
+N_DIRECT = 2
 FLOPS = 2 * 2 * B * H * S * S * D
 DUOS_PER_BATCH = H * NT // 2
 N_DUOS = B * DUOS_PER_BATCH
@@ -35,10 +37,10 @@ def tile_deepseekv4attention_t_kernel(tc, query, key, value, attention_mask, sin
         one = ctx.enter_context(tc.tile_pool(name="one", bufs=1))
         stat = ctx.enter_context(tc.tile_pool(name="stat", bufs=6))
         outp = ctx.enter_context(tc.tile_pool(name="outp", bufs=3))
-        ps_sc = ctx.enter_context(tc.psum_pool(name="ps_sc", bufs=3))
+        ps_sc = ctx.enter_context(tc.psum_pool(name="ps_sc", bufs=4))
         ps_et = ctx.enter_context(tc.psum_pool(name="ps_et", bufs=2))
         ps_o = ctx.enter_context(tc.psum_pool(name="ps_o", bufs=1))
-        ps_tq = ctx.enter_context(tc.psum_pool(name="ps_tq", bufs=2))
+        ps_tq = ctx.enter_context(tc.psum_pool(name="ps_tq", bufs=1))
         ctx.enter_context(tc.manual_schedule())
 
         loaded = {}
@@ -48,6 +50,10 @@ def tile_deepseekv4attention_t_kernel(tc, query, key, value, attention_mask, sin
 
         def valid(n):
             return 0 <= n < N_DUOS
+
+        def mask_on_pe(n):
+            b, j = divmod(n, DUOS_PER_BATCH)
+            return j == DUOS_PER_BATCH - 1 or (j == 3 and b % 2 == 0)
 
         def where(n):
             b, j = divmod(n, DUOS_PER_BATCH)
@@ -153,13 +159,19 @@ def tile_deepseekv4attention_t_kernel(tc, query, key, value, attention_mask, sin
             qTb = ready[b]["q"][:].bitcast(BF16).rearrange("p (c e) -> p c e", e=2)
             kTb = ready[b]["k"][:].bitcast(BF16).rearrange("p (c e) -> p c e", e=2)
             sc = ps_sc.tile([P, S], F32, tag="sc")
-            c0 = (h * NT + 2 * tp + i) * P
+            t = 2 * tp + i
+            c0 = (h * NT + t) * P
+            on_pe = mask_on_pe(n)
+            if on_pe:
+                nc.tensor.matmul(
+                    sc[:], lhsT=ident16[:], rhs=loaded[b]["m"][:, t * S : (t + 1) * S], start=True, stop=False
+                )
             for e in range(2):
                 nc.tensor.matmul(
                     sc[:],
                     lhsT=qTb[:, c0 : c0 + P, e],
                     rhs=kTb[:, g * S : (g + 1) * S, e],
-                    start=(e == 0),
+                    start=(e == 0 and not on_pe),
                     stop=(e == 1),
                 )
             st[(n, "sc", i)] = sc
@@ -169,6 +181,14 @@ def tile_deepseekv4attention_t_kernel(tc, query, key, value, attention_mask, sin
                 return
             b, tp, h = where(n)
             t = 2 * tp + i
+            if mask_on_pe(n):
+                if i == 0:
+                    nm16 = stat.tile([P, 2], F32, tag="nm16")
+                    st[(n, "nm16")] = nm16
+                nc.vector.tensor_reduce(
+                    out=st[(n, "nm16")][:, i : i + 1], in_=st[(n, "sc", i)][:], axis=AX.X, op=ALU.max, negate=True
+                )
+                return
             nc.vector.scalar_tensor_tensor(
                 out=s_bufs[h][:, i, 0:S],
                 in0=st[(n, "sc", i)][:],
@@ -183,7 +203,19 @@ def tile_deepseekv4attention_t_kernel(tc, query, key, value, attention_mask, sin
                 return
             b, tp, h = where(n)
             negm = stat.tile([P, 2], F32, tag="negm")
-            nc.vector.tensor_reduce(out=negm[:], in_=s_bufs[h][:, :, 0 : S + 1], axis=AX.X, op=ALU.max, negate=True)
+            if mask_on_pe(n):
+                nc.vector.tensor_scalar(
+                    out=negm[:],
+                    in0=st[(n, "nm16")][:],
+                    scalar1=1.0 / 16.0,
+                    scalar2=nsink[:, h : h + 1],
+                    op0=ALU.mult,
+                    op1=ALU.min,
+                )
+            else:
+                nc.vector.tensor_reduce(
+                    out=negm[:], in_=s_bufs[h][:, :, 0 : S + 1], axis=AX.X, op=ALU.max, negate=True
+                )
             st[(n, "negm")] = negm
 
         def exps(n):
@@ -192,25 +224,53 @@ def tile_deepseekv4attention_t_kernel(tc, query, key, value, attention_mask, sin
             b, tp, h = where(n)
             negm = st[(n, "negm")]
             e_sb = work.tile([P, 2, SW], BF16, tag="e_sb")
-            den = stat.tile([P, 2], F32, tag="den")
+            if n % 2 == 0:
+                den_pair = stat.tile([P, 2 * DEN_STEP], F32, tag="den_pair")
+                st[(n // 2, "den_pair")] = den_pair
+            c_den = (n % 2) * DEN_STEP
+            if mask_on_pe(n):
+                den = stat.tile([P, 2], F32, tag="den")
+            else:
+                den = st[(n // 2, "den_pair")][:, c_den : c_den + 2]
             for i in range(2):
-                nc.scalar.activation(
-                    out=e_sb[:, i, 0 : S + 1],
-                    in_=s_bufs[h][:, i, 0 : S + 1],
-                    func=ACT.Exp,
-                    bias=negm[:, i : i + 1],
-                    scale=1.0,
-                    accum_out=den[:, i : i + 1],
-                )
+                if mask_on_pe(n):
+                    nc.scalar.activation(
+                        out=e_sb[:, i, 0:S],
+                        in_=st[(n, "sc", i)][:],
+                        func=ACT.Exp,
+                        bias=negm[:, i : i + 1],
+                        scale=1.0 / 16.0,
+                        accum_out=den[:, i : i + 1],
+                    )
+                else:
+                    nc.scalar.activation(
+                        out=e_sb[:, i, 0 : S + 1],
+                        in_=s_bufs[h][:, i, 0 : S + 1],
+                        func=ACT.Exp,
+                        bias=negm[:, i : i + 1],
+                        scale=1.0,
+                        accum_out=den[:, i : i + 1],
+                    )
+            if mask_on_pe(n):
+                sterm = stat.tile([P, 2], F32, tag="sterm")
+                nc.scalar.activation(out=sterm[:], in_=negm[:], func=ACT.Exp, bias=sink_f[:, h : h + 1], scale=1.0)
+                st[(n, "sterm")] = sterm
             st[(n, "e")] = e_sb
             st[(n, "den")] = den
 
         def recip(n):
             if not valid(n):
                 return
-            rden = stat.tile([P, 2], F32, tag="rden")
-            nc.vector.reciprocal(out=rden[:], in_=st[(n, "den")][:])
-            st[(n, "rden")] = rden
+            den_pair = st[(n // 2, "den_pair")]
+            c_den = (n % 2) * DEN_STEP
+            if mask_on_pe(n):
+                nc.vector.tensor_tensor(
+                    out=den_pair[:, c_den : c_den + 2], in0=st[(n, "den")][:], in1=st[(n, "sterm")][:], op=ALU.add
+                )
+            if n % 2 == 1:
+                rden = stat.tile([P, 2, 2], F32, tag="rden")
+                nc.vector.reciprocal(out=rden[:], in_=den_pair[:].rearrange("p (a x) -> p a x", x=DEN_STEP)[:, :, 0:2])
+                st[(n // 2, "rden")] = rden
 
         def e_transposes(n):
             if not valid(n):
@@ -225,21 +285,25 @@ def tile_deepseekv4attention_t_kernel(tc, query, key, value, attention_mask, sin
         def e_out_of_psum(n):
             if not valid(n):
                 return
-            et = st[(n, "et")]
-            etc = work.tile([P, NT * P], BF16, tag="etc")
-            nc.scalar.copy(out=etc[:], in_=et[:, 1].rearrange("p k q -> p (k q)"))
+            if n >= N_DUOS - N_DIRECT:
+                gr_v = work.tile([P, 2 * P * NT], BF16, tag="gr_v", align_bytes=64)
+                nc.vector.tensor_copy(
+                    out=gr_v[:].rearrange("p (i q k) -> p i q k", i=2, k=NT),
+                    in_=st[(n, "et")][:].rearrange("p i k q -> p i q k"),
+                )
+                st[(n, "gr")] = gr_v
+                return
+            etc = work.tile([P, 2 * NT * P], BF16, tag="etc")
+            nc.scalar.copy(out=etc[:], in_=st[(n, "et")][:].rearrange("p i k q -> p (i k q)"))
             st[(n, "etc")] = etc
-            gr_a = work.tile([P, P * NT], BF16, tag="gr_a", align_bytes=64)
-            nc.scalar.copy(out=gr_a[:].rearrange("p (q k) -> p q k", k=NT), in_=et[:, 0].rearrange("p k q -> p q k"))
-            st[(n, "gr_a")] = gr_a
 
         def e_regroup(n):
-            if not valid(n):
+            if not valid(n) or n >= N_DUOS - N_DIRECT:
                 return
-            gr = one.tile([P, P * NT], BF16, tag="gr", align_bytes=64)
+            gr = one.tile([P, 2 * P * NT], BF16, tag="gr", align_bytes=64)
             nc.gpsimd.tensor_scalar(
-                out=gr[:].rearrange("p (q k) -> p q k", k=NT),
-                in0=st[(n, "etc")][:].rearrange("p (k q) -> p q k", k=NT),
+                out=gr[:].rearrange("p (i q k) -> p i q k", i=2, k=NT),
+                in0=st[(n, "etc")][:].rearrange("p (i k q) -> p i q k", i=2, k=NT),
                 scalar1=1.0,
                 scalar2=0.0,
                 op0=ALU.mult,
@@ -252,8 +316,7 @@ def tile_deepseekv4attention_t_kernel(tc, query, key, value, attention_mask, sin
                 return
             ec = work.tile([P, 2 * P], U32, tag="ec", align_bytes=64)
             es = work.tile([P, 2 * P], U8, tag="es", align_bytes=64)
-            nc.vector.quantize_mx(out=ec[:, 0:P].bitcast(FP8X4), scales=es[:, 0:P], in_=st[(n, "gr_a")][:])
-            nc.vector.quantize_mx(out=ec[:, P : 2 * P].bitcast(FP8X4), scales=es[:, P : 2 * P], in_=st[(n, "gr")][:])
+            nc.vector.quantize_mx(out=ec[:].bitcast(FP8X4), scales=es[:], in_=st[(n, "gr")][:])
             st[(n, "ec")] = ec
             st[(n, "es")] = es
 
@@ -284,7 +347,7 @@ def tile_deepseekv4attention_t_kernel(tc, query, key, value, attention_mask, sin
                 return
             b, tp, h = where(n)
             o_ps = st[(n, "o")]
-            rden = st[(n, "rden")]
+            rden = st[(n // 2, "rden")][:, n % 2, :]
             if h == 0:
                 o_new = outp.tile([P, 2, H, D], F32, tag="o_sb")
                 osb[(b, tp)] = o_new
@@ -310,6 +373,12 @@ def tile_deepseekv4attention_t_kernel(tc, query, key, value, attention_mask, sin
         make_identity(nc, ident_f[:])
         ident_b = const.tile([P, P], BF16)
         make_identity(nc, ident_b[:])
+        ident16 = const.tile([P, P], BF16)
+        nc.vector.tensor_scalar(out=ident16[:], in0=ident_b[:], scalar1=16.0, scalar2=None, op0=ALU.mult)
+        sink_f = const.tile([P, H], F32)
+        nc.vector.tensor_copy(out=sink_f[:], in_=sink_raw[:])
+        nsink = const.tile([P, H], F32)
+        nc.vector.tensor_scalar(out=nsink[:], in0=sink_raw[:], scalar1=-1.0, scalar2=None, op0=ALU.mult)
         s_bufs = []
         for h in range(H):
             s_h = const.tile([P, 2, SW], F32, name="s_h%d" % h)
@@ -353,6 +422,6 @@ def tile_deepseekv4attention_t_kernel(tc, query, key, value, attention_mask, sin
             e_regroup(m - 2)
             if valid(m - 1):
                 b1, j1 = divmod(m - 1, DUOS_PER_BATCH)
-                words_copy(b1 + 1, j1 - 2, j1 - 2 == 0)
+                words_copy(b1 + 1, j1 - 2, False)
             if valid(m):
                 words_transpose(b + 1, j - 2)

@@ -17,13 +17,17 @@ G = H // HKV
 P = 128
 NT = S // P
 W = D // 2
-SW = 520
+SCALE = 1.0 / 16.0
+ROW = 520
+UNITS_PER_BATCH = H * NT // 2
+N_UNITS = B * UNITS_PER_BATCH
+TILE_E = P * NT
 DEN_STEP = 8
 N_DIRECT = 2
+WORD_GROUPS = (("k", 0), ("q", 0), ("q", 1), ("k", 1), ("q", 2), ("q", 3))
+FIRST_NEED = {0: (0, 1), 1: (2,), 2: (3, 4), 3: (5,)}
+FIRST_GROUP_ROUND = 2
 FLOPS = 2 * 2 * B * H * S * S * D
-DUOS_PER_BATCH = H * NT // 2
-N_DUOS = B * DUOS_PER_BATCH
-CHUNKS = (("k", 0), ("q", 0), ("q", 1), ("k", 1), ("q", 2), ("q", 3))
 
 
 def tile_deepseekv4attention_t_kernel(tc, query, key, value, attention_mask, sinks, out):
@@ -34,6 +38,7 @@ def tile_deepseekv4attention_t_kernel(tc, query, key, value, attention_mask, sin
         prep = ctx.enter_context(tc.tile_pool(name="prep", bufs=2))
         prep3 = ctx.enter_context(tc.tile_pool(name="prep3", bufs=3))
         work = ctx.enter_context(tc.tile_pool(name="work", bufs=3))
+        work4 = ctx.enter_context(tc.tile_pool(name="work4", bufs=4))
         one = ctx.enter_context(tc.tile_pool(name="one", bufs=1))
         stat = ctx.enter_context(tc.tile_pool(name="stat", bufs=6))
         outp = ctx.enter_context(tc.tile_pool(name="outp", bufs=3))
@@ -46,19 +51,22 @@ def tile_deepseekv4attention_t_kernel(tc, query, key, value, attention_mask, sin
         loaded = {}
         ready = {}
         st = {}
-        osb = {}
 
         def valid(n):
-            return 0 <= n < N_DUOS
-
-        def mask_on_pe(n):
-            b, j = divmod(n, DUOS_PER_BATCH)
-            return j == DUOS_PER_BATCH - 1 or (j == 3 and b % 2 == 0)
+            return 0 <= n < N_UNITS
 
         def where(n):
-            b, j = divmod(n, DUOS_PER_BATCH)
+            b, j = divmod(n, UNITS_PER_BATCH)
             tp, h = divmod(j, H)
             return b, tp, h
+
+        def mask_on_pe(n):
+            b, j = divmod(n, UNITS_PER_BATCH)
+            return j == UNITS_PER_BATCH - 1 or (j == 3 and b % 2 == 0)
+
+        def direct(n):
+            return n >= N_UNITS - N_DIRECT
+
 
         def load(b, fine):
             k_sb = ld.tile([P, HKV * NT * D], BF16, tag="k_sb")
@@ -104,6 +112,7 @@ def tile_deepseekv4attention_t_kernel(tc, query, key, value, attention_mask, sin
                 in_=value[b].rearrange("g (t p) d -> p (g t) d", p=P),
             )
 
+
         def prep_alloc(b):
             qT = prep.tile([P, H * NT * P], F32, tag="qT")
             kT = prep.tile([P, HKV * NT * P], F32, tag="kT")
@@ -113,9 +122,9 @@ def tile_deepseekv4attention_t_kernel(tc, query, key, value, attention_mask, sin
             ready[b] = {"q": qT, "k": kT, "vg": vg, "vc": vc, "vs": vs}
 
         def words_transpose(b, c):
-            if b >= B or not 0 <= c < len(CHUNKS):
+            if b >= B or not 0 <= c < len(WORD_GROUPS):
                 return
-            which, blk = CHUNKS[c]
+            which, blk = WORD_GROUPS[c]
             src = loaded[b][which]
             tq = ps_tq.tile([P, NT, P], F32, tag="tq")
             for t in range(NT):
@@ -124,12 +133,11 @@ def tile_deepseekv4attention_t_kernel(tc, query, key, value, attention_mask, sin
             st[(b, "tq", c)] = tq
 
         def words_copy(b, c, on_vector):
-            if b >= B or not 0 <= c < len(CHUNKS):
+            if b >= B or not 0 <= c < len(WORD_GROUPS):
                 return
-            which, blk = CHUNKS[c]
-            dst = ready[b][which]
+            which, blk = WORD_GROUPS[c]
+            dst_cols = ready[b][which][:, blk * NT * P : (blk + 1) * NT * P]
             tq = st[(b, "tq", c)]
-            dst_cols = dst[:, blk * NT * P : (blk + 1) * NT * P]
             if on_vector:
                 nc.vector.tensor_copy(out=dst_cols, in_=tq[:].rearrange("p t q -> p (t q)"))
             else:
@@ -138,11 +146,10 @@ def tile_deepseekv4attention_t_kernel(tc, query, key, value, attention_mask, sin
         def value_group(b, g):
             if b >= B:
                 return
-            v_sb = loaded[b]["v"]
-            vg = ready[b]["vg"]
+            cols = slice(g * D * NT, (g + 1) * D * NT)
             nc.vector.tensor_copy(
-                out=vg[:, g * D * NT : (g + 1) * D * NT].rearrange("p (c i t) -> p c t i", i=4, t=NT),
-                in_=v_sb[:, g * D * NT : (g + 1) * D * NT].rearrange("p (t c i) -> p c t i", i=4, t=NT),
+                out=ready[b]["vg"][:, cols].rearrange("p (c i t) -> p c t i", i=4, t=NT),
+                in_=loaded[b]["v"][:, cols].rearrange("p (t c i) -> p c t i", i=4, t=NT),
             )
 
         def value_quant(b):
@@ -151,15 +158,16 @@ def tile_deepseekv4attention_t_kernel(tc, query, key, value, attention_mask, sin
             r = ready[b]
             nc.vector.quantize_mx(out=r["vc"][:].bitcast(FP8X4), scales=r["vs"][:], in_=r["vg"][:])
 
+
         def qk(n, i):
             if not valid(n):
                 return
             b, tp, h = where(n)
             g = h // G
+            t = 2 * tp + i
             qTb = ready[b]["q"][:].bitcast(BF16).rearrange("p (c e) -> p c e", e=2)
             kTb = ready[b]["k"][:].bitcast(BF16).rearrange("p (c e) -> p c e", e=2)
             sc = ps_sc.tile([P, S], F32, tag="sc")
-            t = 2 * tp + i
             c0 = (h * NT + t) * P
             on_pe = mask_on_pe(n)
             if on_pe:
@@ -192,7 +200,7 @@ def tile_deepseekv4attention_t_kernel(tc, query, key, value, attention_mask, sin
             nc.vector.scalar_tensor_tensor(
                 out=s_bufs[h][:, i, 0:S],
                 in0=st[(n, "sc", i)][:],
-                scalar=1.0 / 16.0,
+                scalar=SCALE,
                 in1=loaded[b]["m"][:, t * S : (t + 1) * S],
                 op0=ALU.mult,
                 op1=ALU.add,
@@ -207,7 +215,7 @@ def tile_deepseekv4attention_t_kernel(tc, query, key, value, attention_mask, sin
                 nc.vector.tensor_scalar(
                     out=negm[:],
                     in0=st[(n, "nm16")][:],
-                    scalar1=1.0 / 16.0,
+                    scalar1=SCALE,
                     scalar2=nsink[:, h : h + 1],
                     op0=ALU.mult,
                     op1=ALU.min,
@@ -223,7 +231,7 @@ def tile_deepseekv4attention_t_kernel(tc, query, key, value, attention_mask, sin
                 return
             b, tp, h = where(n)
             negm = st[(n, "negm")]
-            e_sb = work.tile([P, 2, SW], BF16, tag="e_sb")
+            e_sb = work.tile([P, 2, ROW], BF16, tag="e_sb")
             if n % 2 == 0:
                 den_pair = stat.tile([P, 2 * DEN_STEP], F32, tag="den_pair")
                 st[(n // 2, "den_pair")] = den_pair
@@ -239,7 +247,7 @@ def tile_deepseekv4attention_t_kernel(tc, query, key, value, attention_mask, sin
                         in_=st[(n, "sc", i)][:],
                         func=ACT.Exp,
                         bias=negm[:, i : i + 1],
-                        scale=1.0 / 16.0,
+                        scale=SCALE,
                         accum_out=den[:, i : i + 1],
                     )
                 else:
@@ -278,47 +286,56 @@ def tile_deepseekv4attention_t_kernel(tc, query, key, value, attention_mask, sin
             e_sb = st[(n, "e")]
             et = ps_et.tile([P, 2, NT, P], BF16, tag="et")
             for i in range(2):
-                for k in range(NT):
-                    nc.tensor.transpose(et[:, i, k, :], e_sb[:, i, k * P : (k + 1) * P], ident_b[:])
+                for t in range(NT):
+                    nc.tensor.transpose(et[:, i, t, :], e_sb[:, i, t * P : (t + 1) * P], ident_b[:])
             st[(n, "et")] = et
 
         def e_out_of_psum(n):
             if not valid(n):
                 return
-            if n >= N_DUOS - N_DIRECT:
-                gr_v = work.tile([P, 2 * P * NT], BF16, tag="gr_v", align_bytes=64)
+            et = st[(n, "et")]
+            if direct(n):
+                gr_v = work.tile([P, 2 * TILE_E], BF16, tag="gr_v", align_bytes=64)
                 nc.vector.tensor_copy(
-                    out=gr_v[:].rearrange("p (i q k) -> p i q k", i=2, k=NT),
-                    in_=st[(n, "et")][:].rearrange("p i k q -> p i q k"),
+                    out=gr_v[:].rearrange("p (i q t) -> p i q t", i=2, t=NT), in_=et[:].rearrange("p i t q -> p i q t")
                 )
-                st[(n, "gr")] = gr_v
+                st[(n, "gr")] = gr_v[:]
                 return
-            etc = work.tile([P, 2 * NT * P], BF16, tag="etc")
-            nc.scalar.copy(out=etc[:], in_=st[(n, "et")][:].rearrange("p i k q -> p (i k q)"))
+            etc = work4.tile([P, 2 * TILE_E], BF16, tag="etc")
+            nc.scalar.copy(out=etc[:], in_=et[:].rearrange("p i t q -> p (i t q)"))
             st[(n, "etc")] = etc
 
         def e_regroup(n):
-            if not valid(n) or n >= N_DUOS - N_DIRECT:
+            if not valid(n) or direct(n):
                 return
-            gr = one.tile([P, 2 * P * NT], BF16, tag="gr", align_bytes=64)
+            if n % 2 == 0:
+                gr = one.tile([P, 4 * TILE_E], BF16, tag="gr", align_bytes=64)
+                st[(n // 2, "gr_pair")] = gr
+            half = st[(n // 2, "gr_pair")][:, (n % 2) * 2 * TILE_E : (n % 2 + 1) * 2 * TILE_E]
             nc.gpsimd.tensor_scalar(
-                out=gr[:].rearrange("p (i q k) -> p i q k", i=2, k=NT),
-                in0=st[(n, "etc")][:].rearrange("p (i k q) -> p i q k", i=2, k=NT),
+                out=half.rearrange("p (i q t) -> p i q t", i=2, t=NT),
+                in0=st[(n, "etc")][:].rearrange("p (i t q) -> p i q t", i=2, t=NT),
                 scalar1=1.0,
                 scalar2=0.0,
                 op0=ALU.mult,
                 op1=ALU.add,
             )
-            st[(n, "gr")] = gr
 
         def e_quant(n):
             if not valid(n):
                 return
-            ec = work.tile([P, 2 * P], U32, tag="ec", align_bytes=64)
-            es = work.tile([P, 2 * P], U8, tag="es", align_bytes=64)
-            nc.vector.quantize_mx(out=ec[:].bitcast(FP8X4), scales=es[:], in_=st[(n, "gr")][:])
-            st[(n, "ec")] = ec
-            st[(n, "es")] = es
+            if n % 2 == 0:
+                ec = work.tile([P, 4 * P], U32, tag="ec", align_bytes=64)
+                es = work.tile([P, 4 * P], U8, tag="es", align_bytes=64)
+                st[(n // 2, "ec")] = ec
+                st[(n // 2, "es")] = es
+            ec = st[(n // 2, "ec")]
+            es = st[(n // 2, "es")]
+            if direct(n):
+                cols = slice((n % 2) * 2 * P, (n % 2 + 1) * 2 * P)
+                nc.vector.quantize_mx(out=ec[:, cols].bitcast(FP8X4), scales=es[:, cols], in_=st[(n, "gr")])
+            elif n % 2 == 1:
+                nc.vector.quantize_mx(out=ec[:].bitcast(FP8X4), scales=es[:], in_=st[(n // 2, "gr_pair")][:])
 
         def pv(n):
             if not valid(n):
@@ -327,14 +344,15 @@ def tile_deepseekv4attention_t_kernel(tc, query, key, value, attention_mask, sin
             g = h // G
             vc = ready[b]["vc"]
             vs = ready[b]["vs"]
-            ec = st[(n, "ec")]
-            es = st[(n, "es")]
+            ec = st[(n // 2, "ec")]
+            es = st[(n // 2, "es")]
             o_ps = ps_o.tile([P, 2, D], F32, tag="o_ps")
             for i in range(2):
+                cols = slice(((n % 2) * 2 + i) * P, ((n % 2) * 2 + i + 1) * P)
                 nc.tensor.matmul_mx(
                     out=o_ps[:, i, :],
-                    lhsT=ec[:, i * P : (i + 1) * P].bitcast(FP8X4),
-                    lhsT_scale=es[:, i * P : (i + 1) * P],
+                    lhsT=ec[:, cols].bitcast(FP8X4),
+                    lhsT_scale=es[:, cols],
                     rhs=vc[:, g * D : (g + 1) * D].bitcast(FP8X4),
                     rhs_scale=vs[:, g * D : (g + 1) * D],
                     start=True,
@@ -350,8 +368,8 @@ def tile_deepseekv4attention_t_kernel(tc, query, key, value, attention_mask, sin
             rden = st[(n // 2, "rden")][:, n % 2, :]
             if h == 0:
                 o_new = outp.tile([P, 2, H, D], F32, tag="o_sb")
-                osb[(b, tp)] = o_new
-            o_sb = osb[(b, tp)]
+                st[(b, tp, "o_sb")] = o_new
+            o_sb = st[(b, tp, "o_sb")]
             for i in range(2):
                 nc.scalar.activation(out=o_sb[:, i, h, :], in_=o_ps[:, i, :], func=ACT.Copy, scale=rden[:, i : i + 1])
             if b == B - 1 and tp == 1:
@@ -365,6 +383,7 @@ def tile_deepseekv4attention_t_kernel(tc, query, key, value, attention_mask, sin
                     in_=o_sb[:].rearrange("p i h d -> p i (h d)"),
                 )
 
+
         sink_raw = const.tile([P, H], BF16)
         nc.scalar.dma_start(out=sink_raw[:], in_=sinks.partition_broadcast(P))
         load(0, True)
@@ -374,22 +393,22 @@ def tile_deepseekv4attention_t_kernel(tc, query, key, value, attention_mask, sin
         ident_b = const.tile([P, P], BF16)
         make_identity(nc, ident_b[:])
         ident16 = const.tile([P, P], BF16)
-        nc.vector.tensor_scalar(out=ident16[:], in0=ident_b[:], scalar1=16.0, scalar2=None, op0=ALU.mult)
+        nc.vector.tensor_scalar(out=ident16[:], in0=ident_b[:], scalar1=1.0 / SCALE, scalar2=None, op0=ALU.mult)
         sink_f = const.tile([P, H], F32)
         nc.vector.tensor_copy(out=sink_f[:], in_=sink_raw[:])
         nsink = const.tile([P, H], F32)
         nc.vector.tensor_scalar(out=nsink[:], in0=sink_raw[:], scalar1=-1.0, scalar2=None, op0=ALU.mult)
         s_bufs = []
         for h in range(H):
-            s_h = const.tile([P, 2, SW], F32, name="s_h%d" % h)
+            s_h = const.tile([P, 2, ROW], F32, name="s_h%d" % h)
             for i in range(2):
                 nc.vector.tensor_copy(out=s_h[:, i, S : S + 1], in_=sink_raw[:, h : h + 1])
             s_bufs.append(s_h)
 
-        first_need = {0: (0, 1), 1: (2,), 2: (3, 4), 3: (5,)}
+
         prep_alloc(0)
-        for m in range(-1, N_DUOS + 4):
-            b, j = divmod(m, DUOS_PER_BATCH)
+        for m in range(-1, N_UNITS + 5):
+            b, j = divmod(m, UNITS_PER_BATCH)
             if valid(m) and j == 0 and b + 2 < B:
                 load(b + 2, False)
             if valid(m) and j == 0 and b + 1 < B:
@@ -397,15 +416,15 @@ def tile_deepseekv4attention_t_kernel(tc, query, key, value, attention_mask, sin
             exps(m - 1)
             add_mask(m, 0)
             add_mask(m, 1)
-            for c in first_need.get(m + 1, ()):
+            for c in FIRST_NEED.get(m + 1, ()):
                 words_transpose(0, c)
                 words_copy(0, c, c % 2 == 1)
             qk(m + 1, 0)
-            pv(m - 4)
+            pv(m - 5)
             qk(m + 1, 1)
             e_out_of_psum(m - 2)
             e_transposes(m - 1)
-            finish(m - 4)
+            finish(m - 5)
             row_max(m)
             if m == 1:
                 value_group(0, 0)
@@ -413,15 +432,15 @@ def tile_deepseekv4attention_t_kernel(tc, query, key, value, attention_mask, sin
                 value_quant(0)
             if valid(m) and j == 2:
                 value_group(b + 1, 0)
-            if valid(m) and j == 3:
-                value_group(b + 1, 1)
             if valid(m) and j == 4:
+                value_group(b + 1, 1)
+            if valid(m) and j == 6:
                 value_quant(b + 1)
             e_quant(m - 3)
             recip(m - 2)
             e_regroup(m - 2)
             if valid(m - 1):
-                b1, j1 = divmod(m - 1, DUOS_PER_BATCH)
-                words_copy(b1 + 1, j1 - 2, False)
+                b1, j1 = divmod(m - 1, UNITS_PER_BATCH)
+                words_copy(b1 + 1, j1 - FIRST_GROUP_ROUND, False)
             if valid(m):
-                words_transpose(b + 1, j - 2)
+                words_transpose(b + 1, j - FIRST_GROUP_ROUND)

from contextlib import ExitStack

import concourse.mybir as mybir
from concourse.masks import make_identity

F32 = mybir.dt.float32
BF16 = mybir.dt.bfloat16
U32 = mybir.dt.uint32
U8 = mybir.dt.uint8
FP8X4 = mybir.dt.float8_e4m3fn_x4
ALU = mybir.AluOpType
ACT = mybir.ActivationFunctionType
AX = mybir.AxisListType

B, H, HKV, S, D = 8, 4, 2, 512, 256
G = H // HKV
P = 128
NT = S // P
W = D // 2
SCALE = 1.0 / 16.0
ROW = 520
UNITS_PER_BATCH = H * NT // 2
N_UNITS = B * UNITS_PER_BATCH
TILE_E = P * NT
DEN_STEP = 8
N_DIRECT = 2
WORD_GROUPS = (("k", 0), ("q", 0), ("q", 1), ("k", 1), ("q", 2), ("q", 3))
FIRST_NEED = {0: (0, 1), 1: (2,), 2: (3, 4), 3: (5,)}
FIRST_GROUP_ROUND = 2
FLOPS = 2 * 2 * B * H * S * S * D


def tile_deepseekv4attention_t_kernel(tc, query, key, value, attention_mask, sinks, out):
    nc = tc.nc
    with ExitStack() as ctx:
        const = ctx.enter_context(tc.tile_pool(name="const", bufs=1))
        ld = ctx.enter_context(tc.tile_pool(name="ld", bufs=3))
        prep = ctx.enter_context(tc.tile_pool(name="prep", bufs=2))
        prep3 = ctx.enter_context(tc.tile_pool(name="prep3", bufs=3))
        work = ctx.enter_context(tc.tile_pool(name="work", bufs=3))
        work4 = ctx.enter_context(tc.tile_pool(name="work4", bufs=4))
        one = ctx.enter_context(tc.tile_pool(name="one", bufs=1))
        stat = ctx.enter_context(tc.tile_pool(name="stat", bufs=6))
        outp = ctx.enter_context(tc.tile_pool(name="outp", bufs=3))
        ps_sc = ctx.enter_context(tc.psum_pool(name="ps_sc", bufs=4))
        ps_et = ctx.enter_context(tc.psum_pool(name="ps_et", bufs=2))
        ps_o = ctx.enter_context(tc.psum_pool(name="ps_o", bufs=1))
        ps_tq = ctx.enter_context(tc.psum_pool(name="ps_tq", bufs=1))
        ctx.enter_context(tc.manual_schedule())

        loaded = {}
        ready = {}
        st = {}

        def valid(n):
            return 0 <= n < N_UNITS

        def where(n):
            b, j = divmod(n, UNITS_PER_BATCH)
            tp, h = divmod(j, H)
            return b, tp, h

        def mask_on_pe(n):
            b, j = divmod(n, UNITS_PER_BATCH)
            return j == UNITS_PER_BATCH - 1 or (j == 3 and b % 2 == 0)

        def direct(n):
            return n >= N_UNITS - N_DIRECT


        def load(b, fine):
            k_sb = ld.tile([P, HKV * NT * D], BF16, tag="k_sb")
            q_sb = ld.tile([P, H * NT * D], BF16, tag="q_sb")
            m_sb = ld.tile([P, NT * S], BF16, tag="m_sb")
            v_sb = ld.tile([P, HKV * NT * D], BF16, tag="v_sb")
            loaded[b] = {"q": q_sb, "k": k_sb, "v": v_sb, "m": m_sb}
            blk = NT * D

            def load_k(g0, g1):
                nc.sync.dma_start(
                    out=k_sb[:, g0 * blk : g1 * blk].rearrange("p (x d) -> p x d", d=D),
                    in_=key[b, g0:g1].rearrange("g (t p) d -> p (g t) d", p=P),
                )

            def load_q(h0, h1):
                nc.sync.dma_start(
                    out=q_sb[:, h0 * blk : h1 * blk].rearrange("p (h x) -> p h x", x=blk),
                    in_=query[b, h0:h1].rearrange("h (p t) d -> p h (t d)", t=NT),
                )

            def load_m(t0, t1):
                nc.sync.dma_start(
                    out=m_sb[:, t0 * S : t1 * S],
                    in_=attention_mask[b, 0].rearrange("(p t) k -> p t k", t=NT)[:, t0:t1, :].rearrange("p t k -> p (t k)"),
                )

            if fine:
                load_k(0, 1)
                load_q(0, 1)
                load_m(0, 2)
                load_q(1, 2)
                load_k(1, 2)
                load_q(2, 3)
                load_q(3, 4)
                load_m(2, NT)
            else:
                load_k(0, HKV)
                load_q(0, H)
                load_m(0, NT)
            nc.sync.dma_start(
                out=v_sb[:].rearrange("p (x d) -> p x d", d=D),
                in_=value[b].rearrange("g (t p) d -> p (g t) d", p=P),
            )


        def prep_alloc(b):
            qT = prep.tile([P, H * NT * P], F32, tag="qT")
            kT = prep.tile([P, HKV * NT * P], F32, tag="kT")
            vg = prep.tile([P, HKV * D * NT], BF16, tag="vg", align_bytes=64)
            vc = prep3.tile([P, HKV * D], U32, tag="vc", align_bytes=64)
            vs = prep3.tile([P, HKV * D], U8, tag="vs", align_bytes=64)
            ready[b] = {"q": qT, "k": kT, "vg": vg, "vc": vc, "vs": vs}

        def words_transpose(b, c):
            if b >= B or not 0 <= c < len(WORD_GROUPS):
                return
            which, blk = WORD_GROUPS[c]
            src = loaded[b][which]
            tq = ps_tq.tile([P, NT, P], F32, tag="tq")
            for t in range(NT):
                c0 = (blk * NT + t) * W
                nc.tensor.transpose(tq[:, t, :], src[:].bitcast(F32)[:, c0 : c0 + W], ident_f[:])
            st[(b, "tq", c)] = tq

        def words_copy(b, c, on_vector):
            if b >= B or not 0 <= c < len(WORD_GROUPS):
                return
            which, blk = WORD_GROUPS[c]
            dst_cols = ready[b][which][:, blk * NT * P : (blk + 1) * NT * P]
            tq = st[(b, "tq", c)]
            if on_vector:
                nc.vector.tensor_copy(out=dst_cols, in_=tq[:].rearrange("p t q -> p (t q)"))
            else:
                nc.scalar.copy(out=dst_cols, in_=tq[:].rearrange("p t q -> p (t q)"))

        def value_group(b, g):
            if b >= B:
                return
            cols = slice(g * D * NT, (g + 1) * D * NT)
            nc.vector.tensor_copy(
                out=ready[b]["vg"][:, cols].rearrange("p (c i t) -> p c t i", i=4, t=NT),
                in_=loaded[b]["v"][:, cols].rearrange("p (t c i) -> p c t i", i=4, t=NT),
            )

        def value_quant(b):
            if b >= B:
                return
            r = ready[b]
            nc.vector.quantize_mx(out=r["vc"][:].bitcast(FP8X4), scales=r["vs"][:], in_=r["vg"][:])


        def qk(n, i):
            if not valid(n):
                return
            b, tp, h = where(n)
            g = h // G
            t = 2 * tp + i
            qTb = ready[b]["q"][:].bitcast(BF16).rearrange("p (c e) -> p c e", e=2)
            kTb = ready[b]["k"][:].bitcast(BF16).rearrange("p (c e) -> p c e", e=2)
            sc = ps_sc.tile([P, S], F32, tag="sc")
            c0 = (h * NT + t) * P
            on_pe = mask_on_pe(n)
            if on_pe:
                nc.tensor.matmul(
                    sc[:], lhsT=ident16[:], rhs=loaded[b]["m"][:, t * S : (t + 1) * S], start=True, stop=False
                )
            for e in range(2):
                nc.tensor.matmul(
                    sc[:],
                    lhsT=qTb[:, c0 : c0 + P, e],
                    rhs=kTb[:, g * S : (g + 1) * S, e],
                    start=(e == 0 and not on_pe),
                    stop=(e == 1),
                )
            st[(n, "sc", i)] = sc

        def add_mask(n, i):
            if not valid(n):
                return
            b, tp, h = where(n)
            t = 2 * tp + i
            if mask_on_pe(n):
                if i == 0:
                    nm16 = stat.tile([P, 2], F32, tag="nm16")
                    st[(n, "nm16")] = nm16
                nc.vector.tensor_reduce(
                    out=st[(n, "nm16")][:, i : i + 1], in_=st[(n, "sc", i)][:], axis=AX.X, op=ALU.max, negate=True
                )
                return
            nc.vector.scalar_tensor_tensor(
                out=s_bufs[h][:, i, 0:S],
                in0=st[(n, "sc", i)][:],
                scalar=SCALE,
                in1=loaded[b]["m"][:, t * S : (t + 1) * S],
                op0=ALU.mult,
                op1=ALU.add,
            )

        def row_max(n):
            if not valid(n):
                return
            b, tp, h = where(n)
            negm = stat.tile([P, 2], F32, tag="negm")
            if mask_on_pe(n):
                nc.vector.tensor_scalar(
                    out=negm[:],
                    in0=st[(n, "nm16")][:],
                    scalar1=SCALE,
                    scalar2=nsink[:, h : h + 1],
                    op0=ALU.mult,
                    op1=ALU.min,
                )
            else:
                nc.vector.tensor_reduce(
                    out=negm[:], in_=s_bufs[h][:, :, 0 : S + 1], axis=AX.X, op=ALU.max, negate=True
                )
            st[(n, "negm")] = negm

        def exps(n):
            if not valid(n):
                return
            b, tp, h = where(n)
            negm = st[(n, "negm")]
            e_sb = work.tile([P, 2, ROW], BF16, tag="e_sb")
            if n % 2 == 0:
                den_pair = stat.tile([P, 2 * DEN_STEP], F32, tag="den_pair")
                st[(n // 2, "den_pair")] = den_pair
            c_den = (n % 2) * DEN_STEP
            if mask_on_pe(n):
                den = stat.tile([P, 2], F32, tag="den")
            else:
                den = st[(n // 2, "den_pair")][:, c_den : c_den + 2]
            for i in range(2):
                if mask_on_pe(n):
                    nc.scalar.activation(
                        out=e_sb[:, i, 0:S],
                        in_=st[(n, "sc", i)][:],
                        func=ACT.Exp,
                        bias=negm[:, i : i + 1],
                        scale=SCALE,
                        accum_out=den[:, i : i + 1],
                    )
                else:
                    nc.scalar.activation(
                        out=e_sb[:, i, 0 : S + 1],
                        in_=s_bufs[h][:, i, 0 : S + 1],
                        func=ACT.Exp,
                        bias=negm[:, i : i + 1],
                        scale=1.0,
                        accum_out=den[:, i : i + 1],
                    )
            if mask_on_pe(n):
                sterm = stat.tile([P, 2], F32, tag="sterm")
                nc.scalar.activation(out=sterm[:], in_=negm[:], func=ACT.Exp, bias=sink_f[:, h : h + 1], scale=1.0)
                st[(n, "sterm")] = sterm
            st[(n, "e")] = e_sb
            st[(n, "den")] = den

        def recip(n):
            if not valid(n):
                return
            den_pair = st[(n // 2, "den_pair")]
            c_den = (n % 2) * DEN_STEP
            if mask_on_pe(n):
                nc.vector.tensor_tensor(
                    out=den_pair[:, c_den : c_den + 2], in0=st[(n, "den")][:], in1=st[(n, "sterm")][:], op=ALU.add
                )
            if n % 2 == 1:
                rden = stat.tile([P, 2, 2], F32, tag="rden")
                nc.vector.reciprocal(out=rden[:], in_=den_pair[:].rearrange("p (a x) -> p a x", x=DEN_STEP)[:, :, 0:2])
                st[(n // 2, "rden")] = rden

        def e_transposes(n):
            if not valid(n):
                return
            e_sb = st[(n, "e")]
            et = ps_et.tile([P, 2, NT, P], BF16, tag="et")
            for i in range(2):
                for t in range(NT):
                    nc.tensor.transpose(et[:, i, t, :], e_sb[:, i, t * P : (t + 1) * P], ident_b[:])
            st[(n, "et")] = et

        def e_out_of_psum(n):
            if not valid(n):
                return
            et = st[(n, "et")]
            if direct(n):
                gr_v = work.tile([P, 2 * TILE_E], BF16, tag="gr_v", align_bytes=64)
                nc.vector.tensor_copy(
                    out=gr_v[:].rearrange("p (i q t) -> p i q t", i=2, t=NT), in_=et[:].rearrange("p i t q -> p i q t")
                )
                st[(n, "gr")] = gr_v[:]
                return
            etc = work4.tile([P, 2 * TILE_E], BF16, tag="etc")
            nc.scalar.copy(out=etc[:], in_=et[:].rearrange("p i t q -> p (i t q)"))
            st[(n, "etc")] = etc

        def e_regroup(n):
            if not valid(n) or direct(n):
                return
            if n % 2 == 0:
                gr = one.tile([P, 4 * TILE_E], BF16, tag="gr", align_bytes=64)
                st[(n // 2, "gr_pair")] = gr
            half = st[(n // 2, "gr_pair")][:, (n % 2) * 2 * TILE_E : (n % 2 + 1) * 2 * TILE_E]
            nc.gpsimd.tensor_scalar(
                out=half.rearrange("p (i q t) -> p i q t", i=2, t=NT),
                in0=st[(n, "etc")][:].rearrange("p (i t q) -> p i q t", i=2, t=NT),
                scalar1=1.0,
                scalar2=0.0,
                op0=ALU.mult,
                op1=ALU.add,
            )

        def e_quant(n):
            if not valid(n):
                return
            if n % 2 == 0:
                ec = work.tile([P, 4 * P], U32, tag="ec", align_bytes=64)
                es = work.tile([P, 4 * P], U8, tag="es", align_bytes=64)
                st[(n // 2, "ec")] = ec
                st[(n // 2, "es")] = es
            ec = st[(n // 2, "ec")]
            es = st[(n // 2, "es")]
            if direct(n):
                cols = slice((n % 2) * 2 * P, (n % 2 + 1) * 2 * P)
                nc.vector.quantize_mx(out=ec[:, cols].bitcast(FP8X4), scales=es[:, cols], in_=st[(n, "gr")])
            elif n % 2 == 1:
                nc.vector.quantize_mx(out=ec[:].bitcast(FP8X4), scales=es[:], in_=st[(n // 2, "gr_pair")][:])

        def pv(n):
            if not valid(n):
                return
            b, tp, h = where(n)
            g = h // G
            vc = ready[b]["vc"]
            vs = ready[b]["vs"]
            ec = st[(n // 2, "ec")]
            es = st[(n // 2, "es")]
            o_ps = ps_o.tile([P, 2, D], F32, tag="o_ps")
            for i in range(2):
                cols = slice(((n % 2) * 2 + i) * P, ((n % 2) * 2 + i + 1) * P)
                nc.tensor.matmul_mx(
                    out=o_ps[:, i, :],
                    lhsT=ec[:, cols].bitcast(FP8X4),
                    lhsT_scale=es[:, cols],
                    rhs=vc[:, g * D : (g + 1) * D].bitcast(FP8X4),
                    rhs_scale=vs[:, g * D : (g + 1) * D],
                    start=True,
                    stop=True,
                )
            st[(n, "o")] = o_ps

        def finish(n):
            if not valid(n):
                return
            b, tp, h = where(n)
            o_ps = st[(n, "o")]
            rden = st[(n // 2, "rden")][:, n % 2, :]
            if h == 0:
                o_new = outp.tile([P, 2, H, D], F32, tag="o_sb")
                st[(b, tp, "o_sb")] = o_new
            o_sb = st[(b, tp, "o_sb")]
            for i in range(2):
                nc.scalar.activation(out=o_sb[:, i, h, :], in_=o_ps[:, i, :], func=ACT.Copy, scale=rden[:, i : i + 1])
            if b == B - 1 and tp == 1:
                nc.sync.dma_start(
                    out=out[b].rearrange("(p t) h d -> p t h d", t=NT)[:, 2 * tp : 2 * tp + 2, h, :],
                    in_=o_sb[:, :, h, :],
                )
            elif h == H - 1:
                nc.sync.dma_start(
                    out=out[b].rearrange("(p t) h d -> p t (h d)", t=NT)[:, 2 * tp : 2 * tp + 2, :],
                    in_=o_sb[:].rearrange("p i h d -> p i (h d)"),
                )


        sink_raw = const.tile([P, H], BF16)
        nc.scalar.dma_start(out=sink_raw[:], in_=sinks.partition_broadcast(P))
        load(0, True)
        load(1, False)
        ident_f = const.tile([P, P], F32)
        make_identity(nc, ident_f[:])
        ident_b = const.tile([P, P], BF16)
        make_identity(nc, ident_b[:])
        ident16 = const.tile([P, P], BF16)
        nc.vector.tensor_scalar(out=ident16[:], in0=ident_b[:], scalar1=1.0 / SCALE, scalar2=None, op0=ALU.mult)
        sink_f = const.tile([P, H], F32)
        nc.vector.tensor_copy(out=sink_f[:], in_=sink_raw[:])
        nsink = const.tile([P, H], F32)
        nc.vector.tensor_scalar(out=nsink[:], in0=sink_raw[:], scalar1=-1.0, scalar2=None, op0=ALU.mult)
        s_bufs = []
        for h in range(H):
            s_h = const.tile([P, 2, ROW], F32, name="s_h%d" % h)
            for i in range(2):
                nc.vector.tensor_copy(out=s_h[:, i, S : S + 1], in_=sink_raw[:, h : h + 1])
            s_bufs.append(s_h)


        prep_alloc(0)
        for m in range(-1, N_UNITS + 5):
            b, j = divmod(m, UNITS_PER_BATCH)
            if valid(m) and j == 0 and b + 2 < B:
                load(b + 2, False)
            if valid(m) and j == 0 and b + 1 < B:
                prep_alloc(b + 1)
            exps(m - 1)
            add_mask(m, 0)
            add_mask(m, 1)
            for c in FIRST_NEED.get(m + 1, ()):
                words_transpose(0, c)
                words_copy(0, c, c % 2 == 1)
            qk(m + 1, 0)
            pv(m - 5)
            qk(m + 1, 1)
            e_out_of_psum(m - 2)
            e_transposes(m - 1)
            finish(m - 5)
            row_max(m)
            if m == 1:
                value_group(0, 0)
                value_group(0, 1)
                value_quant(0)
            if valid(m) and j == 2:
                value_group(b + 1, 0)
            if valid(m) and j == 4:
                value_group(b + 1, 1)
            if valid(m) and j == 6:
                value_quant(b + 1)
            e_quant(m - 3)
            recip(m - 2)
            e_regroup(m - 2)
            if valid(m - 1):
                b1, j1 = divmod(m - 1, UNITS_PER_BATCH)
                words_copy(b1 + 1, j1 - FIRST_GROUP_ROUND, False)
            if valid(m):
                words_transpose(b + 1, j - FIRST_GROUP_ROUND)
